import numpy as np
import ml_dtypes


def mxq(x, axis, fmt="e4m3"):
    dtype, down = {"e4m3": (ml_dtypes.float8_e4m3fn, 7), "e5m2": (ml_dtypes.float8_e5m2, 14)}[fmt]
    v = np.moveaxis(np.asarray(x, np.float32).astype(ml_dtypes.bfloat16).astype(np.float64), axis, -1)
    blocks = v.reshape(v.shape[:-1] + (-1, 32))
    amax = np.abs(blocks).max(-1, keepdims=True)
    byte = np.maximum(np.where(amax > 0, np.frexp(amax)[1] - 1 + 127, 0) - down, 1)
    scale = np.exp2(byte - 127.0)
    codes = (blocks / scale).astype(np.float32).astype(dtype).astype(np.float64)
    return np.moveaxis((codes * scale).reshape(v.shape), -1, axis)


WIDE = False


def mx_kscale(k):
    if not WIDE:
        return np.ones(k)
    levels = np.array([20, -20, 10, -10, 0])
    a = np.random.permutation(np.resize(levels, k // 512 * 4)).reshape(k // 512, 4)
    idx = np.arange(k)
    return np.exp2(a[idx // 512, idx % 128 // 32])


BF16 = ml_dtypes.bfloat16


def bf(x):
    return np.asarray(x, np.float32).astype(BF16)


def f64(x):
    return np.asarray(x).astype(np.float64)


B, N, C0, C1, C2, O0, O1, O2 = 16, 16, 512, 512, 512, 512, 2048, 512
G = C1 + C2
K = 2 * G
T = B * N * N


def sigmoid(v):
    return 1.0 / (1.0 + np.exp(-v))


def preact(x1, x2, W2, b2):
    x1, x2 = f64(x1), f64(x2)
    e1 = np.broadcast_to(x1[:, :, None, :], (B, N, N, C1))
    g = np.concatenate([e1, x2], axis=-1)
    f2 = np.concatenate([g, np.swapaxes(g, 1, 2)], axis=-1)
    return f2 @ f64(W2) + f64(b2)


def setup_inputs():
    u = mx_kscale(O2)
    x1 = bf(np.random.random((B, N, C1)))
    x2 = bf(np.random.random((B, N, N, C2)))
    W20 = bf(np.random.standard_normal((K, O2)) * 2.0 / np.sqrt(K))
    b2 = bf(np.random.standard_normal(O2) * 0.3)
    g = bf(np.random.standard_normal((B, N, N, O2)) * np.exp2(np.random.randint(-12, 1, (B, N, N, 1))) * 16.0 * u)
    z = preact(x1, x2, W20, b2)
    return {"x1": x1, "x2": x2, "W2": bf(f64(W20) / u[None, :]), "b2": b2,
            "z": np.asarray(z, np.float32), "grad_out": g}


def reference(x1, x2, W2, b2, z, grad_out):
    sg = sigmoid(f64(z))
    dz = f64(grad_out) * (sg * (1.0 - sg))
    dq = mxq(dz.reshape(T, O2), 1, "e5m2")
    W = f64(W2)
    wb = mxq(W[C1:G], 1, "e4m3")
    wd = mxq(W[G + C1:K], 1, "e4m3")
    p = (dq @ wb.T).reshape(B, N, N, C2)
    q = (dq @ wd.T).reshape(B, N, N, C2)
    return p + np.swapaxes(q, 1, 2)

@@ -1,0 +1,242 @@
+from contextlib import ExitStack
+
+import concourse.mybir as mybir
+from concourse.masks import make_identity
+
+F32 = mybir.dt.float32
+BF16 = mybir.dt.bfloat16
+I32 = mybir.dt.int32
+U32 = mybir.dt.uint32
+U8 = mybir.dt.uint8
+E5M2X4 = mybir.dt.float8_e5m2_x4
+E4M3X4 = mybir.dt.float8_e4m3fn_x4
+ACT = mybir.ActivationFunctionType
+ALU = mybir.AluOpType
+
+P = 128
+PACK = 4
+SCENES = 16
+OBJECTS = 16
+CHANNELS = 512
+OUT_CHANNELS = 512
+
+GROUP_SCENES = 4
+GROUPS = SCENES // GROUP_SCENES
+GROUP_TOKENS = GROUP_SCENES * OBJECTS * OBJECTS
+BLOCKS = GROUP_TOKENS // P
+UNIT_BLOCKS = 2
+UNITS = BLOCKS // UNIT_BLOCKS
+UNIT_TOKENS = UNIT_BLOCKS * P
+HALF_BLOCKS = BLOCKS // 2
+HALF_TOKENS = HALF_BLOCKS * P
+ROWS_OF_A_SCENE = P // GROUP_SCENES
+
+LOAD_BUFS = 12
+LEAD_UNITS = 2
+
+FLOPS = 2 * 2 * SCENES * OBJECTS * OBJECTS * CHANNELS * OUT_CHANNELS
+BYTES = SCENES * OBJECTS * OBJECTS * (CHANNELS * (4 + 2) + OUT_CHANNELS * 4) + 2 * OUT_CHANNELS * CHANNELS * 2
+
+
+def tile_differentiablelogicmachine_pa_v_kernel(tc, x1, x2, W2, b2, z, grad_out, out):
+    nc = tc.nc
+
+    z_units = z.rearrange("b i j o -> (b i j) o").rearrange(
+        "(q p u r) o -> q u p r o", q=GROUPS, p=P, u=UNITS, r=UNIT_BLOCKS
+    )
+    g_units = grad_out.rearrange("b i j o -> (b i j) o").rearrange(
+        "(q p u r) o -> q u p r o", q=GROUPS, p=P, u=UNITS, r=UNIT_BLOCKS
+    )
+    out_halves = out.rearrange("b i j c -> (b i j) c").rearrange(
+        "(s x h r) c -> s h x r c", s=SCENES, x=ROWS_OF_A_SCENE, h=2, r=HALF_BLOCKS
+    )
+
+    with ExitStack() as ctx:
+        consts = ctx.enter_context(tc.tile_pool(name="consts", bufs=1))
+        weights = ctx.enter_context(tc.tile_pool(name="weights", bufs=1))
+        loads = ctx.enter_context(tc.tile_pool(name="loads", bufs=LOAD_BUFS))
+        work = ctx.enter_context(tc.tile_pool(name="work", bufs=3))
+        regroup = ctx.enter_context(tc.tile_pool(name="regroup", bufs=2))
+        keep = ctx.enter_context(tc.tile_pool(name="keep", bufs=1))
+        results = ctx.enter_context(tc.tile_pool(name="results", bufs=4))
+        psum_z = ctx.enter_context(tc.psum_pool(name="psum_z", bufs=3))
+        psum_g = ctx.enter_context(tc.psum_pool(name="psum_g", bufs=2))
+        psum_o = ctx.enter_context(tc.psum_pool(name="psum_o", bufs=3))
+
+        z_tiles = {}
+        g_tiles = {}
+
+        def load_unit(q, u):
+            z_tile = loads.tile([P, UNIT_BLOCKS, CHANNELS], F32)
+            nc.sync.dma_start(out=z_tile[:], in_=z_units[q, u])
+            g_tile = loads.tile([P, UNIT_BLOCKS, CHANNELS], BF16)
+            nc.sync.dma_start(out=g_tile[:], in_=g_units[q, u])
+            z_tiles[(q, u)] = z_tile
+            g_tiles[(q, u)] = g_tile
+
+        def load_weight(first_row, name):
+            w_rows = weights.tile([P, OUT_CHANNELS // P, CHANNELS], BF16, name=name)
+            nc.sync.dma_start(
+                out=w_rows[:],
+                in_=W2[first_row : first_row + OUT_CHANNELS, :].rearrange("(n p) o -> p n o", p=P),
+            )
+            return w_rows
+
+        all_units = [(q, u) for q in range(GROUPS) for u in range(UNITS)]
+        for q, u in all_units[:LEAD_UNITS]:
+            load_unit(q, u)
+        wb_rows = load_weight(512, "wb_rows")
+        wd_rows = load_weight(1536, "wd_rows")
+        for q, u in all_units[LEAD_UNITS:]:
+            load_unit(q, u)
+
+        ident_f32 = consts.tile([P, P], F32)
+        make_identity(nc, ident_f32[:])
+        ident_bf = consts.tile([P, P], BF16)
+        nc.vector.tensor_copy(out=ident_bf[:], in_=ident_f32[:])
+        perm_f32 = consts.tile([P, P], F32)
+        perm_bf = consts.tile([P, P], BF16)
+        for perm in (perm_f32, perm_bf):
+            nc.vector.tensor_copy(
+                out=perm[:].rearrange("p (x s) -> p x s", s=GROUP_SCENES),
+                in_=ident_f32[:].rearrange("p (s x) -> p x s", s=GROUP_SCENES),
+            )
+
+        dz_codes = keep.tile([P, GROUPS, GROUP_TOKENS], U32, align_bytes=64)
+        dz_scales = keep.tile([P, GROUPS, GROUP_TOKENS], U8, align_bytes=64)
+        swap_codes = keep.tile([P, GROUPS, GROUP_TOKENS], U32, align_bytes=64)
+        swap_scales = keep.tile([P, GROUPS, GROUP_TOKENS], U8, align_bytes=64)
+        nc.vector.memset(dz_scales[:].rearrange("p q n -> p (q n)").bitcast(I32), 0)
+
+        wb_codes = keep.tile([P, OUT_CHANNELS], U32, align_bytes=64)
+        wb_scales = keep.tile([P, OUT_CHANNELS], U8, align_bytes=64)
+        wd_codes = keep.tile([P, OUT_CHANNELS], U32, align_bytes=64)
+        wd_scales = keep.tile([P, OUT_CHANNELS], U8, align_bytes=64)
+
+        def quantise_weight(w_rows, codes, scales, name):
+            w_grouped = weights.tile([P, OUT_CHANNELS, PACK], BF16, align_bytes=64, name=name)
+            for half in range(2):
+                wT = psum_g.tile([P, PACK, UNIT_TOKENS], BF16, tag="bf16_bank")
+                for n in range(2):
+                    for t in range(PACK):
+                        nc.tensor.transpose(
+                            wT[:, t, n * P : (n + 1) * P],
+                            w_rows[:, 2 * half + n, t * P : (t + 1) * P],
+                            ident_bf[:],
+                        )
+                nc.scalar.copy(
+                    out=w_grouped[:, half * UNIT_TOKENS : (half + 1) * UNIT_TOKENS, :],
+                    in_=wT[:].rearrange("p t c -> p c t"),
+                )
+            nc.vector.quantize_mx(
+                out=codes[:].bitcast(E4M3X4),
+                scales=scales[:],
+                in_=w_grouped[:].rearrange("p c t -> p (c t)"),
+            )
+
+        grouped_tiles = {}
+
+        def gradient_unit(q, u):
+            if u == 0:
+                grouped = regroup.tile([P, GROUP_TOKENS, PACK], BF16, align_bytes=64)
+                grouped_tiles[q] = grouped
+            grouped = grouped_tiles[q]
+            z_tile = z_tiles[(q, u)]
+            g_tile = g_tiles[(q, u)]
+
+            slope = work.tile([P, PACK, UNIT_TOKENS], F32)
+            for r in range(UNIT_BLOCKS):
+                zT = psum_z.tile([P, PACK, P], F32)
+                for t in range(PACK):
+                    nc.tensor.transpose(zT[:, t, :], z_tile[:, r, t * P : (t + 1) * P], perm_f32[:])
+                nc.scalar.activation(out=slope[:, :, r * P : (r + 1) * P], in_=zT[:], func=ACT.Sigmoid)
+            gT = psum_g.tile([P, PACK, UNIT_TOKENS], BF16, tag="bf16_bank")
+            for r in range(UNIT_BLOCKS):
+                for t in range(PACK):
+                    nc.tensor.transpose(
+                        gT[:, t, r * P : (r + 1) * P], g_tile[:, r, t * P : (t + 1) * P], perm_bf[:]
+                    )
+            flat = slope[:].rearrange("p t c -> p (t c)")
+            nc.vector.scalar_tensor_tensor(
+                out=flat, in0=flat, scalar=1.0, in1=flat, op0=ALU.subtract, op1=ALU.mult
+            )
+            nc.vector.scalar_tensor_tensor(
+                out=grouped[:, u * UNIT_TOKENS : (u + 1) * UNIT_TOKENS, :],
+                in0=slope[:].rearrange("p t c -> p c t"),
+                scalar=-1.0,
+                in1=gT[:].rearrange("p t c -> p c t"),
+                op0=ALU.mult,
+                op1=ALU.mult,
+            )
+            if u % 2 == 1:
+                half = slice((u // 2) * HALF_TOKENS, (u // 2 + 1) * HALF_TOKENS)
+                nc.vector.quantize_mx(
+                    out=dz_codes[:, q, half].bitcast(E5M2X4),
+                    scales=dz_scales[:, q, half],
+                    in_=grouped[:, half, :].rearrange("p c t -> p (c t)"),
+                )
+            if u == UNITS - 1:
+                swap_objects(q)
+
+        def swap_objects(q):
+            split = "p (jl ih il jh s) -> p jl ih il jh s"
+            sizes = dict(jl=8, ih=2, il=8, jh=2)
+            src = dz_codes[:, q, :].bitcast(I32).rearrange(split, s=GROUP_SCENES, **sizes)
+            dst = swap_codes[:, q, :].bitcast(I32).rearrange(split, s=GROUP_SCENES, **sizes)
+            for ih in range(2):
+                nc.vector.tensor_copy(
+                    out=dst[:, :, ih, :, :, :],
+                    in_=src[:, :, :, :, ih, :].rearrange("p il jh jl s -> p jl il jh s"),
+                )
+            src = dz_scales[:, q, :].bitcast(I32).rearrange("p (jl ih il jh) -> p jl ih il jh", **sizes)
+            dst = swap_scales[:, q, :].bitcast(I32).rearrange("p (jl ih il jh) -> p jl ih il jh", **sizes)
+            nc.vector.tensor_copy(out=dst, in_=src.rearrange("p il jh jl ih -> p jl ih il jh"))
+
+        result_tiles = {}
+
+        def product_unit(q, u):
+            if u % 2 == 0:
+                result = results.tile([P, HALF_BLOCKS, OUT_CHANNELS], F32)
+                result_tiles[q] = result
+            result = result_tiles[q]
+            for r in range(UNIT_BLOCKS):
+                block = u * UNIT_BLOCKS + r
+                cols = slice(block * P, (block + 1) * P)
+                acc = psum_o.tile([P, OUT_CHANNELS], F32)
+                nc.tensor.matmul_mx(
+                    out=acc[:],
+                    lhsT=dz_codes[:, q, cols].bitcast(E5M2X4),
+                    lhsT_scale=dz_scales[:, q, cols],
+                    rhs=wb_codes[:].bitcast(E4M3X4),
+                    rhs_scale=wb_scales[:],
+                    start=True,
+                    stop=False,
+                )
+                nc.tensor.matmul_mx(
+                    out=acc[:],
+                    lhsT=swap_codes[:, q, cols].bitcast(E5M2X4),
+                    lhsT_scale=swap_scales[:, q, cols],
+                    rhs=wd_codes[:].bitcast(E4M3X4),
+                    rhs_scale=wd_scales[:],
+                    start=False,
+                    stop=True,
+                )
+                nc.scalar.copy(out=result[:, block % HALF_BLOCKS, :], in_=acc[:])
+            if u % 2 == 1:
+                for s in range(GROUP_SCENES):
+                    nc.sync.dma_start(
+                        out=out_halves[q * GROUP_SCENES + s, u // 2],
+                        in_=result[s:P:GROUP_SCENES, :, :],
+                    )
+
+        for u in range(UNITS):
+            gradient_unit(0, u)
+            if u == LEAD_UNITS - 1:
+                quantise_weight(wb_rows, wb_codes, wb_scales, "wb_grouped")
+                quantise_weight(wd_rows, wd_codes, wd_scales, "wd_grouped")
+        for q in range(1, GROUPS):
+            for u in range(UNITS):
+                gradient_unit(q, u)
+                product_unit(q - 1, u)
+        for u in range(UNITS):
+            product_unit(GROUPS - 1, u)

@@ -48,7 +48,7 @@ def tile_differentiablelogicmachine_pa_v_kernel(tc, x1, x2, W2, b2, z, grad_out,
         "(q p u r) o -> q u p r o", q=GROUPS, p=P, u=UNITS, r=UNIT_BLOCKS
     )
     out_halves = out.rearrange("b i j c -> (b i j) c").rearrange(
-        "(s x h r) c -> s h x r c", s=SCENES, x=ROWS_OF_A_SCENE, h=2, r=HALF_BLOCKS
+        "(q s x h r) c -> q h x s (r c)", q=GROUPS, s=GROUP_SCENES, x=ROWS_OF_A_SCENE, h=2, r=HALF_BLOCKS
     )
 
     with ExitStack() as ctx:
@@ -223,11 +223,10 @@ def tile_differentiablelogicmachine_pa_v_kernel(tc, x1, x2, W2, b2, z, grad_out,
                 )
                 nc.scalar.copy(out=result[:, block % HALF_BLOCKS, :], in_=acc[:])
             if u % 2 == 1:
-                for s in range(GROUP_SCENES):
-                    nc.sync.dma_start(
-                        out=out_halves[q * GROUP_SCENES + s, u // 2],
-                        in_=result[s:P:GROUP_SCENES, :, :],
-                    )
+                nc.sync.dma_start(
+                    out=out_halves[q, u // 2],
+                    in_=result[:].rearrange("p r c -> p (r c)"),
+                )
 
         for u in range(UNITS):
             gradient_unit(0, u)

@@ -23,16 +23,21 @@ OUT_CHANNELS = 512
 GROUP_SCENES = 4
 GROUPS = SCENES // GROUP_SCENES
 GROUP_TOKENS = GROUP_SCENES * OBJECTS * OBJECTS
-BLOCKS = GROUP_TOKENS // P
+GROUP_BLOCKS = GROUP_TOKENS // P
+BLOCKS = GROUPS * GROUP_BLOCKS
 UNIT_BLOCKS = 2
-UNITS = BLOCKS // UNIT_BLOCKS
 UNIT_TOKENS = UNIT_BLOCKS * P
-HALF_BLOCKS = BLOCKS // 2
+UNITS = BLOCKS // UNIT_BLOCKS
+GROUP_UNITS = GROUP_BLOCKS // UNIT_BLOCKS
+HALF_BLOCKS = GROUP_BLOCKS // 2
+HALF_UNITS = HALF_BLOCKS // UNIT_BLOCKS
 HALF_TOKENS = HALF_BLOCKS * P
 ROWS_OF_A_SCENE = P // GROUP_SCENES
 
 LOAD_BUFS = 12
 LEAD_UNITS = 2
+WEIGHT_BANKS = 2
+LAG_BLOCKS = GROUP_BLOCKS + 6
 
 FLOPS = 2 * 2 * SCENES * OBJECTS * OBJECTS * CHANNELS * OUT_CHANNELS
 BYTES = SCENES * OBJECTS * OBJECTS * (CHANNELS * (4 + 2) + OUT_CHANNELS * 4) + 2 * OUT_CHANNELS * CHANNELS * 2
@@ -42,53 +47,27 @@ def tile_differentiablelogicmachine_pa_v_kernel(tc, x1, x2, W2, b2, z, grad_out,
     nc = tc.nc
 
     z_units = z.rearrange("b i j o -> (b i j) o").rearrange(
-        "(q p u r) o -> q u p r o", q=GROUPS, p=P, u=UNITS, r=UNIT_BLOCKS
+        "(q p u r) o -> q u p r o", q=GROUPS, p=P, u=GROUP_UNITS, r=UNIT_BLOCKS
     )
     g_units = grad_out.rearrange("b i j o -> (b i j) o").rearrange(
-        "(q p u r) o -> q u p r o", q=GROUPS, p=P, u=UNITS, r=UNIT_BLOCKS
+        "(q p u r) o -> q u p r o", q=GROUPS, p=P, u=GROUP_UNITS, r=UNIT_BLOCKS
     )
     out_halves = out.rearrange("b i j c -> (b i j) c").rearrange(
         "(q s x h r) c -> q h x s (r c)", q=GROUPS, s=GROUP_SCENES, x=ROWS_OF_A_SCENE, h=2, r=HALF_BLOCKS
     )
 
     with ExitStack() as ctx:
+        ctx.enter_context(tc.manual_schedule())
         consts = ctx.enter_context(tc.tile_pool(name="consts", bufs=1))
         weights = ctx.enter_context(tc.tile_pool(name="weights", bufs=1))
         loads = ctx.enter_context(tc.tile_pool(name="loads", bufs=LOAD_BUFS))
         work = ctx.enter_context(tc.tile_pool(name="work", bufs=3))
-        regroup = ctx.enter_context(tc.tile_pool(name="regroup", bufs=2))
+        regroup = ctx.enter_context(tc.tile_pool(name="regroup", bufs=3))
         keep = ctx.enter_context(tc.tile_pool(name="keep", bufs=1))
         results = ctx.enter_context(tc.tile_pool(name="results", bufs=4))
         psum_z = ctx.enter_context(tc.psum_pool(name="psum_z", bufs=3))
         psum_g = ctx.enter_context(tc.psum_pool(name="psum_g", bufs=2))
         psum_o = ctx.enter_context(tc.psum_pool(name="psum_o", bufs=3))
-
-        z_tiles = {}
-        g_tiles = {}
-
-        def load_unit(q, u):
-            z_tile = loads.tile([P, UNIT_BLOCKS, CHANNELS], F32)
-            nc.sync.dma_start(out=z_tile[:], in_=z_units[q, u])
-            g_tile = loads.tile([P, UNIT_BLOCKS, CHANNELS], BF16)
-            nc.sync.dma_start(out=g_tile[:], in_=g_units[q, u])
-            z_tiles[(q, u)] = z_tile
-            g_tiles[(q, u)] = g_tile
-
-        def load_weight(first_row, name):
-            w_rows = weights.tile([P, OUT_CHANNELS // P, CHANNELS], BF16, name=name)
-            nc.sync.dma_start(
-                out=w_rows[:],
-                in_=W2[first_row : first_row + OUT_CHANNELS, :].rearrange("(n p) o -> p n o", p=P),
-            )
-            return w_rows
-
-        all_units = [(q, u) for q in range(GROUPS) for u in range(UNITS)]
-        for q, u in all_units[:LEAD_UNITS]:
-            load_unit(q, u)
-        wb_rows = load_weight(512, "wb_rows")
-        wd_rows = load_weight(1536, "wd_rows")
-        for q, u in all_units[LEAD_UNITS:]:
-            load_unit(q, u)
 
         ident_f32 = consts.tile([P, P], F32)
         make_identity(nc, ident_f32[:])
@@ -102,6 +81,33 @@ def tile_differentiablelogicmachine_pa_v_kernel(tc, x1, x2, W2, b2, z, grad_out,
                 in_=ident_f32[:].rearrange("p (s x) -> p x s", s=GROUP_SCENES),
             )
 
+        z_tiles = []
+        g_tiles = []
+
+        def load_unit(unit):
+            q, u = divmod(unit, GROUP_UNITS)
+            z_tile = loads.tile([P, UNIT_BLOCKS, CHANNELS], F32)
+            nc.sync.dma_start(out=z_tile[:], in_=z_units[q, u])
+            g_tile = loads.tile([P, UNIT_BLOCKS, CHANNELS], BF16)
+            nc.sync.dma_start(out=g_tile[:], in_=g_units[q, u])
+            z_tiles.append(z_tile)
+            g_tiles.append(g_tile)
+
+        def load_weight(first_row, name):
+            w_rows = weights.tile([P, OUT_CHANNELS // P, CHANNELS], BF16, name=name)
+            nc.sync.dma_start(
+                out=w_rows[:],
+                in_=W2[first_row : first_row + OUT_CHANNELS, :].rearrange("(n p) o -> p n o", p=P),
+            )
+            return w_rows
+
+        for unit in range(LEAD_UNITS):
+            load_unit(unit)
+        wb_rows = load_weight(512, "wb_rows")
+        wd_rows = load_weight(1536, "wd_rows")
+        for unit in range(LEAD_UNITS, UNITS):
+            load_unit(unit)
+
         dz_codes = keep.tile([P, GROUPS, GROUP_TOKENS], U32, align_bytes=64)
         dz_scales = keep.tile([P, GROUPS, GROUP_TOKENS], U8, align_bytes=64)
         swap_codes = keep.tile([P, GROUPS, GROUP_TOKENS], U32, align_bytes=64)
@@ -113,70 +119,84 @@ def tile_differentiablelogicmachine_pa_v_kernel(tc, x1, x2, W2, b2, z, grad_out,
         wd_codes = keep.tile([P, OUT_CHANNELS], U32, align_bytes=64)
         wd_scales = keep.tile([P, OUT_CHANNELS], U8, align_bytes=64)
 
-        def quantise_weight(w_rows, codes, scales, name):
-            w_grouped = weights.tile([P, OUT_CHANNELS, PACK], BF16, align_bytes=64, name=name)
-            for half in range(2):
-                wT = psum_g.tile([P, PACK, UNIT_TOKENS], BF16, tag="bf16_bank")
-                for n in range(2):
-                    for t in range(PACK):
-                        nc.tensor.transpose(
-                            wT[:, t, n * P : (n + 1) * P],
-                            w_rows[:, 2 * half + n, t * P : (t + 1) * P],
-                            ident_bf[:],
-                        )
-                nc.scalar.copy(
-                    out=w_grouped[:, half * UNIT_TOKENS : (half + 1) * UNIT_TOKENS, :],
-                    in_=wT[:].rearrange("p t c -> p c t"),
-                )
-            nc.vector.quantize_mx(
-                out=codes[:].bitcast(E4M3X4),
-                scales=scales[:],
-                in_=w_grouped[:].rearrange("p c t -> p (c t)"),
-            )
+        wb_grouped = weights.tile([P, OUT_CHANNELS, PACK], BF16, align_bytes=64)
+        wd_grouped = weights.tile([P, OUT_CHANNELS, PACK], BF16, align_bytes=64)
+        weight_operands = (
+            (wb_rows, wb_grouped, wb_codes, wb_scales),
+            (wd_rows, wd_grouped, wd_codes, wd_scales),
+        )
 
-        grouped_tiles = {}
-
-        def gradient_unit(q, u):
-            if u == 0:
-                grouped = regroup.tile([P, GROUP_TOKENS, PACK], BF16, align_bytes=64)
-                grouped_tiles[q] = grouped
-            grouped = grouped_tiles[q]
-            z_tile = z_tiles[(q, u)]
-            g_tile = g_tiles[(q, u)]
-
-            slope = work.tile([P, PACK, UNIT_TOKENS], F32)
-            for r in range(UNIT_BLOCKS):
-                zT = psum_z.tile([P, PACK, P], F32)
-                for t in range(PACK):
-                    nc.tensor.transpose(zT[:, t, :], z_tile[:, r, t * P : (t + 1) * P], perm_f32[:])
-                nc.scalar.activation(out=slope[:, :, r * P : (r + 1) * P], in_=zT[:], func=ACT.Sigmoid)
-            gT = psum_g.tile([P, PACK, UNIT_TOKENS], BF16, tag="bf16_bank")
-            for r in range(UNIT_BLOCKS):
+        def weight_bank(index):
+            w_rows, w_grouped, codes, scales = weight_operands[index // WEIGHT_BANKS]
+            bank = index % WEIGHT_BANKS
+            wT = psum_o.tile([P, PACK, UNIT_TOKENS], BF16, tag="acc")
+            for n in range(2):
                 for t in range(PACK):
                     nc.tensor.transpose(
-                        gT[:, t, r * P : (r + 1) * P], g_tile[:, r, t * P : (t + 1) * P], perm_bf[:]
+                        wT[:, t, n * P : (n + 1) * P],
+                        w_rows[:, 2 * bank + n, t * P : (t + 1) * P],
+                        ident_bf[:],
                     )
-            flat = slope[:].rearrange("p t c -> p (t c)")
+            nc.scalar.copy(
+                out=w_grouped[:, bank * UNIT_TOKENS : (bank + 1) * UNIT_TOKENS, :],
+                in_=wT[:].rearrange("p t c -> p c t"),
+            )
+            if bank == WEIGHT_BANKS - 1:
+                nc.vector.quantize_mx(
+                    out=codes[:].bitcast(E4M3X4),
+                    scales=scales[:],
+                    in_=w_grouped[:].rearrange("p c t -> p (c t)"),
+                )
+
+        slope_tiles = {}
+        gT_tiles = {}
+        grouped_tiles = {}
+
+        def transpose_block(block):
+            unit, r = divmod(block, UNIT_BLOCKS)
+            if r == 0:
+                slope = work.tile([P, PACK, UNIT_TOKENS], F32)
+                gT = psum_g.tile([P, PACK, UNIT_TOKENS], BF16, tag="bf16_bank")
+                slope_tiles[unit] = slope
+                gT_tiles[unit] = gT
+            cols = slice(r * P, (r + 1) * P)
+            zT = psum_z.tile([P, PACK, P], F32)
+            for t in range(PACK):
+                nc.tensor.transpose(zT[:, t, :], z_tiles[unit][:, r, t * P : (t + 1) * P], perm_f32[:])
+            for t in range(PACK):
+                nc.tensor.transpose(
+                    gT_tiles[unit][:, t, cols], g_tiles[unit][:, r, t * P : (t + 1) * P], perm_bf[:]
+                )
+            nc.scalar.activation(out=slope_tiles[unit][:, :, cols], in_=zT[:], func=ACT.Sigmoid)
+
+        def sigmoid_slope(unit):
+            flat = slope_tiles[unit][:].rearrange("p t c -> p (t c)")
             nc.vector.scalar_tensor_tensor(
                 out=flat, in0=flat, scalar=1.0, in1=flat, op0=ALU.subtract, op1=ALU.mult
             )
+
+        def gradient(unit):
+            half, n = divmod(unit, HALF_UNITS)
+            if n == 0:
+                grouped = regroup.tile([P, HALF_TOKENS, PACK], BF16, align_bytes=64)
+                grouped_tiles[half] = grouped
             nc.vector.scalar_tensor_tensor(
-                out=grouped[:, u * UNIT_TOKENS : (u + 1) * UNIT_TOKENS, :],
-                in0=slope[:].rearrange("p t c -> p c t"),
+                out=grouped_tiles[half][:, n * UNIT_TOKENS : (n + 1) * UNIT_TOKENS, :],
+                in0=slope_tiles[unit][:].rearrange("p t c -> p c t"),
                 scalar=-1.0,
-                in1=gT[:].rearrange("p t c -> p c t"),
+                in1=gT_tiles[unit][:].rearrange("p t c -> p c t"),
                 op0=ALU.mult,
                 op1=ALU.mult,
             )
-            if u % 2 == 1:
-                half = slice((u // 2) * HALF_TOKENS, (u // 2 + 1) * HALF_TOKENS)
-                nc.vector.quantize_mx(
-                    out=dz_codes[:, q, half].bitcast(E5M2X4),
-                    scales=dz_scales[:, q, half],
-                    in_=grouped[:, half, :].rearrange("p c t -> p (c t)"),
-                )
-            if u == UNITS - 1:
-                swap_objects(q)
+
+        def quantise_half(half):
+            q, h = divmod(half, 2)
+            cols = slice(h * HALF_TOKENS, (h + 1) * HALF_TOKENS)
+            nc.vector.quantize_mx(
+                out=dz_codes[:, q, cols].bitcast(E5M2X4),
+                scales=dz_scales[:, q, cols],
+                in_=grouped_tiles[half][:].rearrange("p c t -> p (c t)"),
+            )
 
         def swap_objects(q):
             split = "p (jl ih il jh s) -> p jl ih il jh s"
@@ -194,48 +214,55 @@ def tile_differentiablelogicmachine_pa_v_kernel(tc, x1, x2, W2, b2, z, grad_out,
 
         result_tiles = {}
 
-        def product_unit(q, u):
-            if u % 2 == 0:
+        def product_block(block):
+            q, n = divmod(block, GROUP_BLOCKS)
+            half, r = divmod(block, HALF_BLOCKS)
+            if r == 0:
                 result = results.tile([P, HALF_BLOCKS, OUT_CHANNELS], F32)
-                result_tiles[q] = result
-            result = result_tiles[q]
-            for r in range(UNIT_BLOCKS):
-                block = u * UNIT_BLOCKS + r
-                cols = slice(block * P, (block + 1) * P)
-                acc = psum_o.tile([P, OUT_CHANNELS], F32)
-                nc.tensor.matmul_mx(
-                    out=acc[:],
-                    lhsT=dz_codes[:, q, cols].bitcast(E5M2X4),
-                    lhsT_scale=dz_scales[:, q, cols],
-                    rhs=wb_codes[:].bitcast(E4M3X4),
-                    rhs_scale=wb_scales[:],
-                    start=True,
-                    stop=False,
-                )
-                nc.tensor.matmul_mx(
-                    out=acc[:],
-                    lhsT=swap_codes[:, q, cols].bitcast(E5M2X4),
-                    lhsT_scale=swap_scales[:, q, cols],
-                    rhs=wd_codes[:].bitcast(E4M3X4),
-                    rhs_scale=wd_scales[:],
-                    start=False,
-                    stop=True,
-                )
-                nc.scalar.copy(out=result[:, block % HALF_BLOCKS, :], in_=acc[:])
-            if u % 2 == 1:
+                result_tiles[half] = result
+            cols = slice(n * P, (n + 1) * P)
+            acc = psum_o.tile([P, OUT_CHANNELS], F32, tag="acc")
+            nc.tensor.matmul_mx(
+                out=acc[:],
+                lhsT=dz_codes[:, q, cols].bitcast(E5M2X4),
+                lhsT_scale=dz_scales[:, q, cols],
+                rhs=wb_codes[:].bitcast(E4M3X4),
+                rhs_scale=wb_scales[:],
+                start=True,
+                stop=False,
+            )
+            nc.tensor.matmul_mx(
+                out=acc[:],
+                lhsT=swap_codes[:, q, cols].bitcast(E5M2X4),
+                lhsT_scale=swap_scales[:, q, cols],
+                rhs=wd_codes[:].bitcast(E4M3X4),
+                rhs_scale=wd_scales[:],
+                start=False,
+                stop=True,
+            )
+            nc.scalar.copy(out=result_tiles[half][:, r, :], in_=acc[:])
+            if r == HALF_BLOCKS - 1:
                 nc.sync.dma_start(
-                    out=out_halves[q, u // 2],
-                    in_=result[:].rearrange("p r c -> p (r c)"),
+                    out=out_halves[q, half % 2], in_=result_tiles[half][:].rearrange("p r c -> p (r c)")
                 )
 
-        for u in range(UNITS):
-            gradient_unit(0, u)
-            if u == LEAD_UNITS - 1:
-                quantise_weight(wb_rows, wb_codes, wb_scales, "wb_grouped")
-                quantise_weight(wd_rows, wd_codes, wd_scales, "wd_grouped")
-        for q in range(1, GROUPS):
-            for u in range(UNITS):
-                gradient_unit(q, u)
-                product_unit(q - 1, u)
-        for u in range(UNITS):
-            product_unit(GROUPS - 1, u)
+        def vector_round(unit):
+            if unit < UNITS:
+                sigmoid_slope(unit)
+            if unit > 0 and unit % HALF_UNITS == 0:
+                quantise_half(unit // HALF_UNITS - 1)
+            if unit < UNITS:
+                gradient(unit)
+            if unit > 0 and unit % GROUP_UNITS == 0:
+                swap_objects(unit // GROUP_UNITS - 1)
+
+        for step in range(BLOCKS + LAG_BLOCKS):
+            unit, r = divmod(step, UNIT_BLOCKS)
+            if step < BLOCKS:
+                transpose_block(step)
+            if r == UNIT_BLOCKS - 1 and unit <= UNITS:
+                vector_round(unit)
+            if r == UNIT_BLOCKS - 1 and 0 <= unit + 1 - LEAD_UNITS < 2 * WEIGHT_BANKS:
+                weight_bank(unit + 1 - LEAD_UNITS)
+            if step >= LAG_BLOCKS:
+                product_block(step - LAG_BLOCKS)

@@ -32,12 +32,14 @@ GROUP_UNITS = GROUP_BLOCKS // UNIT_BLOCKS
 HALF_BLOCKS = GROUP_BLOCKS // 2
 HALF_UNITS = HALF_BLOCKS // UNIT_BLOCKS
 HALF_TOKENS = HALF_BLOCKS * P
+STORE_BLOCKS = 2
+GROUP_STORES = GROUP_BLOCKS // STORE_BLOCKS
 ROWS_OF_A_SCENE = P // GROUP_SCENES
 
 LOAD_BUFS = 12
-LEAD_UNITS = 2
+LEAD_UNITS = 4
 WEIGHT_BANKS = 2
-LAG_BLOCKS = GROUP_BLOCKS + 6
+LAG_BLOCKS = GROUP_BLOCKS + 8
 
 FLOPS = 2 * 2 * SCENES * OBJECTS * OBJECTS * CHANNELS * OUT_CHANNELS
 BYTES = SCENES * OBJECTS * OBJECTS * (CHANNELS * (4 + 2) + OUT_CHANNELS * 4) + 2 * OUT_CHANNELS * CHANNELS * 2
@@ -52,8 +54,8 @@ def tile_differentiablelogicmachine_pa_v_kernel(tc, x1, x2, W2, b2, z, grad_out,
     g_units = grad_out.rearrange("b i j o -> (b i j) o").rearrange(
         "(q p u r) o -> q u p r o", q=GROUPS, p=P, u=GROUP_UNITS, r=UNIT_BLOCKS
     )
-    out_halves = out.rearrange("b i j c -> (b i j) c").rearrange(
-        "(q s x h r) c -> q h x s (r c)", q=GROUPS, s=GROUP_SCENES, x=ROWS_OF_A_SCENE, h=2, r=HALF_BLOCKS
+    out_stores = out.rearrange("b i j c -> (b i j) c").rearrange(
+        "(q s x n r) c -> q n x s (r c)", q=GROUPS, s=GROUP_SCENES, x=ROWS_OF_A_SCENE, n=GROUP_STORES, r=STORE_BLOCKS
     )
 
     with ExitStack() as ctx:
@@ -64,7 +66,7 @@ def tile_differentiablelogicmachine_pa_v_kernel(tc, x1, x2, W2, b2, z, grad_out,
         work = ctx.enter_context(tc.tile_pool(name="work", bufs=3))
         regroup = ctx.enter_context(tc.tile_pool(name="regroup", bufs=3))
         keep = ctx.enter_context(tc.tile_pool(name="keep", bufs=1))
-        results = ctx.enter_context(tc.tile_pool(name="results", bufs=4))
+        results = ctx.enter_context(tc.tile_pool(name="results", bufs=6))
         psum_z = ctx.enter_context(tc.psum_pool(name="psum_z", bufs=3))
         psum_g = ctx.enter_context(tc.psum_pool(name="psum_g", bufs=2))
         psum_o = ctx.enter_context(tc.psum_pool(name="psum_o", bufs=3))
@@ -148,16 +150,17 @@ def tile_differentiablelogicmachine_pa_v_kernel(tc, x1, x2, W2, b2, z, grad_out,
                     in_=w_grouped[:].rearrange("p c t -> p (c t)"),
                 )
 
-        slope_tiles = {}
+        sigmoid_tiles = {}
         gT_tiles = {}
+        weighted_tiles = {}
         grouped_tiles = {}
 
         def transpose_block(block):
             unit, r = divmod(block, UNIT_BLOCKS)
             if r == 0:
-                slope = work.tile([P, PACK, UNIT_TOKENS], F32)
-                gT = psum_g.tile([P, PACK, UNIT_TOKENS], BF16, tag="bf16_bank")
-                slope_tiles[unit] = slope
+                sigmoid = work.tile([P, UNIT_TOKENS, PACK], F32)
+                gT = psum_g.tile([P, PACK, UNIT_TOKENS], BF16)
+                sigmoid_tiles[unit] = sigmoid
                 gT_tiles[unit] = gT
             cols = slice(r * P, (r + 1) * P)
             zT = psum_z.tile([P, PACK, P], F32)
@@ -167,12 +170,20 @@ def tile_differentiablelogicmachine_pa_v_kernel(tc, x1, x2, W2, b2, z, grad_out,
                 nc.tensor.transpose(
                     gT_tiles[unit][:, t, cols], g_tiles[unit][:, r, t * P : (t + 1) * P], perm_bf[:]
                 )
-            nc.scalar.activation(out=slope_tiles[unit][:, :, cols], in_=zT[:], func=ACT.Sigmoid)
+            nc.scalar.activation(
+                out=sigmoid_tiles[unit][:, cols, :], in_=zT[:].rearrange("p t c -> p c t"), func=ACT.Sigmoid
+            )
 
-        def sigmoid_slope(unit):
-            flat = slope_tiles[unit][:].rearrange("p t c -> p (t c)")
+        def weigh(unit):
+            weighted = work.tile([P, UNIT_TOKENS, PACK], F32)
+            weighted_tiles[unit] = weighted
             nc.vector.scalar_tensor_tensor(
-                out=flat, in0=flat, scalar=1.0, in1=flat, op0=ALU.subtract, op1=ALU.mult
+                out=weighted[:],
+                in0=sigmoid_tiles[unit][:],
+                scalar=-1.0,
+                in1=gT_tiles[unit][:].rearrange("p t c -> p c t"),
+                op0=ALU.mult,
+                op1=ALU.mult,
             )
 
         def gradient(unit):
@@ -182,10 +193,10 @@ def tile_differentiablelogicmachine_pa_v_kernel(tc, x1, x2, W2, b2, z, grad_out,
                 grouped_tiles[half] = grouped
             nc.vector.scalar_tensor_tensor(
                 out=grouped_tiles[half][:, n * UNIT_TOKENS : (n + 1) * UNIT_TOKENS, :],
-                in0=slope_tiles[unit][:].rearrange("p t c -> p c t"),
-                scalar=-1.0,
-                in1=gT_tiles[unit][:].rearrange("p t c -> p c t"),
-                op0=ALU.mult,
+                in0=sigmoid_tiles[unit][:],
+                scalar=1.0,
+                in1=weighted_tiles[unit][:],
+                op0=ALU.subtract,
                 op1=ALU.mult,
             )
 
@@ -216,10 +227,10 @@ def tile_differentiablelogicmachine_pa_v_kernel(tc, x1, x2, W2, b2, z, grad_out,
 
         def product_block(block):
             q, n = divmod(block, GROUP_BLOCKS)
-            half, r = divmod(block, HALF_BLOCKS)
+            store, r = divmod(block, STORE_BLOCKS)
             if r == 0:
-                result = results.tile([P, HALF_BLOCKS, OUT_CHANNELS], F32)
-                result_tiles[half] = result
+                result = results.tile([P, STORE_BLOCKS, OUT_CHANNELS], F32)
+                result_tiles[store] = result
             cols = slice(n * P, (n + 1) * P)
             acc = psum_o.tile([P, OUT_CHANNELS], F32, tag="acc")
             nc.tensor.matmul_mx(
@@ -240,27 +251,29 @@ def tile_differentiablelogicmachine_pa_v_kernel(tc, x1, x2, W2, b2, z, grad_out,
                 start=False,
                 stop=True,
             )
-            nc.scalar.copy(out=result_tiles[half][:, r, :], in_=acc[:])
-            if r == HALF_BLOCKS - 1:
+            nc.scalar.copy(out=result_tiles[store][:, r, :], in_=acc[:])
+            if r == STORE_BLOCKS - 1:
                 nc.sync.dma_start(
-                    out=out_halves[q, half % 2], in_=result_tiles[half][:].rearrange("p r c -> p (r c)")
+                    out=out_stores[q, store % GROUP_STORES],
+                    in_=result_tiles[store][:].rearrange("p r c -> p (r c)"),
                 )
 
         def vector_round(unit):
+            finished = unit - 1
             if unit < UNITS:
-                sigmoid_slope(unit)
-            if unit > 0 and unit % HALF_UNITS == 0:
-                quantise_half(unit // HALF_UNITS - 1)
-            if unit < UNITS:
-                gradient(unit)
-            if unit > 0 and unit % GROUP_UNITS == 0:
-                swap_objects(unit // GROUP_UNITS - 1)
+                weigh(unit)
+            if finished > 0 and finished % HALF_UNITS == 0:
+                quantise_half(finished // HALF_UNITS - 1)
+            if 0 <= finished < UNITS:
+                gradient(finished)
+            if finished > 0 and finished % GROUP_UNITS == 0:
+                swap_objects(finished // GROUP_UNITS - 1)
 
         for step in range(BLOCKS + LAG_BLOCKS):
             unit, r = divmod(step, UNIT_BLOCKS)
             if step < BLOCKS:
                 transpose_block(step)
-            if r == UNIT_BLOCKS - 1 and unit <= UNITS:
+            if r == UNIT_BLOCKS - 1 and unit <= UNITS + 1:
                 vector_round(unit)
             if r == UNIT_BLOCKS - 1 and 0 <= unit + 1 - LEAD_UNITS < 2 * WEIGHT_BANKS:
                 weight_bank(unit + 1 - LEAD_UNITS)

@@ -19,6 +19,8 @@ SCENES = 16
 OBJECTS = 16
 CHANNELS = 512
 OUT_CHANNELS = 512
+WB_FIRST_ROW = 512
+WD_FIRST_ROW = 1536
 
 GROUP_SCENES = 4
 GROUPS = SCENES // GROUP_SCENES
@@ -29,17 +31,25 @@ UNIT_BLOCKS = 2
 UNIT_TOKENS = UNIT_BLOCKS * P
 UNITS = BLOCKS // UNIT_BLOCKS
 GROUP_UNITS = GROUP_BLOCKS // UNIT_BLOCKS
-HALF_BLOCKS = GROUP_BLOCKS // 2
-HALF_UNITS = HALF_BLOCKS // UNIT_BLOCKS
-HALF_TOKENS = HALF_BLOCKS * P
+GROUP_HALVES = 2
+HALF_UNITS = GROUP_UNITS // GROUP_HALVES
+HALF_TOKENS = GROUP_TOKENS // GROUP_HALVES
 STORE_BLOCKS = 2
 GROUP_STORES = GROUP_BLOCKS // STORE_BLOCKS
-ROWS_OF_A_SCENE = P // GROUP_SCENES
+PAIRS = P // GROUP_SCENES
+WEIGHT_CHUNKS = OUT_CHANNELS // P
+BANK_CHUNKS = 2
+WEIGHT_BANKS = WEIGHT_CHUNKS // BANK_CHUNKS
 
 LOAD_BUFS = 12
 LEAD_UNITS = 4
-WEIGHT_BANKS = 2
-LAG_BLOCKS = GROUP_BLOCKS + 8
+WORK_BUFS = 3
+REGROUP_BUFS = 3
+RESULT_BUFS = 6
+Z_BANKS = 3
+G_BANKS = 2
+OUT_BANKS = 3
+LAG_UNITS = GROUP_UNITS + 2 + G_BANKS
 
 FLOPS = 2 * 2 * SCENES * OBJECTS * OBJECTS * CHANNELS * OUT_CHANNELS
 BYTES = SCENES * OBJECTS * OBJECTS * (CHANNELS * (4 + 2) + OUT_CHANNELS * 4) + 2 * OUT_CHANNELS * CHANNELS * 2
@@ -55,7 +65,7 @@ def tile_differentiablelogicmachine_pa_v_kernel(tc, x1, x2, W2, b2, z, grad_out,
         "(q p u r) o -> q u p r o", q=GROUPS, p=P, u=GROUP_UNITS, r=UNIT_BLOCKS
     )
     out_stores = out.rearrange("b i j c -> (b i j) c").rearrange(
-        "(q s x n r) c -> q n x s (r c)", q=GROUPS, s=GROUP_SCENES, x=ROWS_OF_A_SCENE, n=GROUP_STORES, r=STORE_BLOCKS
+        "(q s x n r) c -> q n x s (r c)", q=GROUPS, s=GROUP_SCENES, x=PAIRS, n=GROUP_STORES, r=STORE_BLOCKS
     )
 
     with ExitStack() as ctx:
@@ -63,13 +73,13 @@ def tile_differentiablelogicmachine_pa_v_kernel(tc, x1, x2, W2, b2, z, grad_out,
         consts = ctx.enter_context(tc.tile_pool(name="consts", bufs=1))
         weights = ctx.enter_context(tc.tile_pool(name="weights", bufs=1))
         loads = ctx.enter_context(tc.tile_pool(name="loads", bufs=LOAD_BUFS))
-        work = ctx.enter_context(tc.tile_pool(name="work", bufs=3))
-        regroup = ctx.enter_context(tc.tile_pool(name="regroup", bufs=3))
+        work = ctx.enter_context(tc.tile_pool(name="work", bufs=WORK_BUFS))
+        regroup = ctx.enter_context(tc.tile_pool(name="regroup", bufs=REGROUP_BUFS))
         keep = ctx.enter_context(tc.tile_pool(name="keep", bufs=1))
-        results = ctx.enter_context(tc.tile_pool(name="results", bufs=6))
-        psum_z = ctx.enter_context(tc.psum_pool(name="psum_z", bufs=3))
-        psum_g = ctx.enter_context(tc.psum_pool(name="psum_g", bufs=2))
-        psum_o = ctx.enter_context(tc.psum_pool(name="psum_o", bufs=3))
+        results = ctx.enter_context(tc.tile_pool(name="results", bufs=RESULT_BUFS))
+        psum_z = ctx.enter_context(tc.psum_pool(name="psum_z", bufs=Z_BANKS))
+        psum_g = ctx.enter_context(tc.psum_pool(name="psum_g", bufs=G_BANKS))
+        psum_o = ctx.enter_context(tc.psum_pool(name="psum_o", bufs=OUT_BANKS))
 
         ident_f32 = consts.tile([P, P], F32)
         make_identity(nc, ident_f32[:])
@@ -87,16 +97,16 @@ def tile_differentiablelogicmachine_pa_v_kernel(tc, x1, x2, W2, b2, z, grad_out,
         g_tiles = []
 
         def load_unit(unit):
-            q, u = divmod(unit, GROUP_UNITS)
+            group, unit_in_group = divmod(unit, GROUP_UNITS)
             z_tile = loads.tile([P, UNIT_BLOCKS, CHANNELS], F32)
-            nc.sync.dma_start(out=z_tile[:], in_=z_units[q, u])
+            nc.sync.dma_start(out=z_tile[:], in_=z_units[group, unit_in_group])
             g_tile = loads.tile([P, UNIT_BLOCKS, CHANNELS], BF16)
-            nc.sync.dma_start(out=g_tile[:], in_=g_units[q, u])
+            nc.sync.dma_start(out=g_tile[:], in_=g_units[group, unit_in_group])
             z_tiles.append(z_tile)
             g_tiles.append(g_tile)
 
         def load_weight(first_row, name):
-            w_rows = weights.tile([P, OUT_CHANNELS // P, CHANNELS], BF16, name=name)
+            w_rows = weights.tile([P, WEIGHT_CHUNKS, CHANNELS], BF16, name=name)
             nc.sync.dma_start(
                 out=w_rows[:],
                 in_=W2[first_row : first_row + OUT_CHANNELS, :].rearrange("(n p) o -> p n o", p=P),
@@ -105,8 +115,8 @@ def tile_differentiablelogicmachine_pa_v_kernel(tc, x1, x2, W2, b2, z, grad_out,
 
         for unit in range(LEAD_UNITS):
             load_unit(unit)
-        wb_rows = load_weight(512, "wb_rows")
-        wd_rows = load_weight(1536, "wd_rows")
+        wb_rows = load_weight(WB_FIRST_ROW, "wb_rows")
+        wd_rows = load_weight(WD_FIRST_ROW, "wd_rows")
         for unit in range(LEAD_UNITS, UNITS):
             load_unit(unit)
 
@@ -132,11 +142,11 @@ def tile_differentiablelogicmachine_pa_v_kernel(tc, x1, x2, W2, b2, z, grad_out,
             w_rows, w_grouped, codes, scales = weight_operands[index // WEIGHT_BANKS]
             bank = index % WEIGHT_BANKS
             wT = psum_o.tile([P, PACK, UNIT_TOKENS], BF16, tag="acc")
-            for n in range(2):
+            for n in range(BANK_CHUNKS):
                 for t in range(PACK):
                     nc.tensor.transpose(
                         wT[:, t, n * P : (n + 1) * P],
-                        w_rows[:, 2 * bank + n, t * P : (t + 1) * P],
+                        w_rows[:, BANK_CHUNKS * bank + n, t * P : (t + 1) * P],
                         ident_bf[:],
                     )
             nc.scalar.copy(
@@ -156,19 +166,19 @@ def tile_differentiablelogicmachine_pa_v_kernel(tc, x1, x2, W2, b2, z, grad_out,
         grouped_tiles = {}
 
         def transpose_block(block):
-            unit, r = divmod(block, UNIT_BLOCKS)
-            if r == 0:
+            unit, part = divmod(block, UNIT_BLOCKS)
+            if part == 0:
                 sigmoid = work.tile([P, UNIT_TOKENS, PACK], F32)
                 gT = psum_g.tile([P, PACK, UNIT_TOKENS], BF16)
                 sigmoid_tiles[unit] = sigmoid
                 gT_tiles[unit] = gT
-            cols = slice(r * P, (r + 1) * P)
+            cols = slice(part * P, (part + 1) * P)
             zT = psum_z.tile([P, PACK, P], F32)
             for t in range(PACK):
-                nc.tensor.transpose(zT[:, t, :], z_tiles[unit][:, r, t * P : (t + 1) * P], perm_f32[:])
+                nc.tensor.transpose(zT[:, t, :], z_tiles[unit][:, part, t * P : (t + 1) * P], perm_f32[:])
             for t in range(PACK):
                 nc.tensor.transpose(
-                    gT_tiles[unit][:, t, cols], g_tiles[unit][:, r, t * P : (t + 1) * P], perm_bf[:]
+                    gT_tiles[unit][:, t, cols], g_tiles[unit][:, part, t * P : (t + 1) * P], perm_bf[:]
                 )
             nc.scalar.activation(
                 out=sigmoid_tiles[unit][:, cols, :], in_=zT[:].rearrange("p t c -> p c t"), func=ACT.Sigmoid
@@ -187,12 +197,12 @@ def tile_differentiablelogicmachine_pa_v_kernel(tc, x1, x2, W2, b2, z, grad_out,
             )
 
         def gradient(unit):
-            half, n = divmod(unit, HALF_UNITS)
-            if n == 0:
+            half, unit_in_half = divmod(unit, HALF_UNITS)
+            if unit_in_half == 0:
                 grouped = regroup.tile([P, HALF_TOKENS, PACK], BF16, align_bytes=64)
                 grouped_tiles[half] = grouped
             nc.vector.scalar_tensor_tensor(
-                out=grouped_tiles[half][:, n * UNIT_TOKENS : (n + 1) * UNIT_TOKENS, :],
+                out=grouped_tiles[half][:, unit_in_half * UNIT_TOKENS : (unit_in_half + 1) * UNIT_TOKENS, :],
                 in0=sigmoid_tiles[unit][:],
                 scalar=1.0,
                 in1=weighted_tiles[unit][:],
@@ -201,42 +211,42 @@ def tile_differentiablelogicmachine_pa_v_kernel(tc, x1, x2, W2, b2, z, grad_out,
             )
 
         def quantise_half(half):
-            q, h = divmod(half, 2)
-            cols = slice(h * HALF_TOKENS, (h + 1) * HALF_TOKENS)
+            group, side = divmod(half, GROUP_HALVES)
+            cols = slice(side * HALF_TOKENS, (side + 1) * HALF_TOKENS)
             nc.vector.quantize_mx(
-                out=dz_codes[:, q, cols].bitcast(E5M2X4),
-                scales=dz_scales[:, q, cols],
+                out=dz_codes[:, group, cols].bitcast(E5M2X4),
+                scales=dz_scales[:, group, cols],
                 in_=grouped_tiles[half][:].rearrange("p c t -> p (c t)"),
             )
 
-        def swap_objects(q):
+        def swap_objects(group):
             split = "p (jl ih il jh s) -> p jl ih il jh s"
             sizes = dict(jl=8, ih=2, il=8, jh=2)
-            src = dz_codes[:, q, :].bitcast(I32).rearrange(split, s=GROUP_SCENES, **sizes)
-            dst = swap_codes[:, q, :].bitcast(I32).rearrange(split, s=GROUP_SCENES, **sizes)
+            src = dz_codes[:, group, :].bitcast(I32).rearrange(split, s=GROUP_SCENES, **sizes)
+            dst = swap_codes[:, group, :].bitcast(I32).rearrange(split, s=GROUP_SCENES, **sizes)
             for ih in range(2):
                 nc.vector.tensor_copy(
                     out=dst[:, :, ih, :, :, :],
                     in_=src[:, :, :, :, ih, :].rearrange("p il jh jl s -> p jl il jh s"),
                 )
-            src = dz_scales[:, q, :].bitcast(I32).rearrange("p (jl ih il jh) -> p jl ih il jh", **sizes)
-            dst = swap_scales[:, q, :].bitcast(I32).rearrange("p (jl ih il jh) -> p jl ih il jh", **sizes)
+            src = dz_scales[:, group, :].bitcast(I32).rearrange("p (jl ih il jh) -> p jl ih il jh", **sizes)
+            dst = swap_scales[:, group, :].bitcast(I32).rearrange("p (jl ih il jh) -> p jl ih il jh", **sizes)
             nc.vector.tensor_copy(out=dst, in_=src.rearrange("p il jh jl ih -> p jl ih il jh"))
 
         result_tiles = {}
 
         def product_block(block):
-            q, n = divmod(block, GROUP_BLOCKS)
-            store, r = divmod(block, STORE_BLOCKS)
-            if r == 0:
+            group, block_in_group = divmod(block, GROUP_BLOCKS)
+            store, slot = divmod(block, STORE_BLOCKS)
+            if slot == 0:
                 result = results.tile([P, STORE_BLOCKS, OUT_CHANNELS], F32)
                 result_tiles[store] = result
-            cols = slice(n * P, (n + 1) * P)
+            cols = slice(block_in_group * P, (block_in_group + 1) * P)
             acc = psum_o.tile([P, OUT_CHANNELS], F32, tag="acc")
             nc.tensor.matmul_mx(
                 out=acc[:],
-                lhsT=dz_codes[:, q, cols].bitcast(E5M2X4),
-                lhsT_scale=dz_scales[:, q, cols],
+                lhsT=dz_codes[:, group, cols].bitcast(E5M2X4),
+                lhsT_scale=dz_scales[:, group, cols],
                 rhs=wb_codes[:].bitcast(E4M3X4),
                 rhs_scale=wb_scales[:],
                 start=True,
@@ -244,17 +254,17 @@ def tile_differentiablelogicmachine_pa_v_kernel(tc, x1, x2, W2, b2, z, grad_out,
             )
             nc.tensor.matmul_mx(
                 out=acc[:],
-                lhsT=swap_codes[:, q, cols].bitcast(E5M2X4),
-                lhsT_scale=swap_scales[:, q, cols],
+                lhsT=swap_codes[:, group, cols].bitcast(E5M2X4),
+                lhsT_scale=swap_scales[:, group, cols],
                 rhs=wd_codes[:].bitcast(E4M3X4),
                 rhs_scale=wd_scales[:],
                 start=False,
                 stop=True,
             )
-            nc.scalar.copy(out=result_tiles[store][:, r, :], in_=acc[:])
-            if r == STORE_BLOCKS - 1:
+            nc.scalar.copy(out=result_tiles[store][:, slot, :], in_=acc[:])
+            if slot == STORE_BLOCKS - 1:
                 nc.sync.dma_start(
-                    out=out_stores[q, store % GROUP_STORES],
+                    out=out_stores[group, store % GROUP_STORES],
                     in_=result_tiles[store][:].rearrange("p r c -> p (r c)"),
                 )
 
@@ -269,13 +279,14 @@ def tile_differentiablelogicmachine_pa_v_kernel(tc, x1, x2, W2, b2, z, grad_out,
             if finished > 0 and finished % GROUP_UNITS == 0:
                 swap_objects(finished // GROUP_UNITS - 1)
 
-        for step in range(BLOCKS + LAG_BLOCKS):
-            unit, r = divmod(step, UNIT_BLOCKS)
-            if step < BLOCKS:
-                transpose_block(step)
-            if r == UNIT_BLOCKS - 1 and unit <= UNITS + 1:
+        for unit in range(UNITS + LAG_UNITS):
+            if unit < UNITS:
+                for part in range(UNIT_BLOCKS):
+                    transpose_block(unit * UNIT_BLOCKS + part)
+            if unit <= UNITS + 1:
                 vector_round(unit)
-            if r == UNIT_BLOCKS - 1 and 0 <= unit + 1 - LEAD_UNITS < 2 * WEIGHT_BANKS:
+            if 0 <= unit + 1 - LEAD_UNITS < 2 * WEIGHT_BANKS:
                 weight_bank(unit + 1 - LEAD_UNITS)
-            if step >= LAG_BLOCKS:
-                product_block(step - LAG_BLOCKS)
+            if unit >= LAG_UNITS:
+                for part in range(UNIT_BLOCKS):
+                    product_block((unit - LAG_UNITS) * UNIT_BLOCKS + part)

@@ -51,6 +51,11 @@ G_BANKS = 2
 OUT_BANKS = 3
 LAG_UNITS = GROUP_UNITS + 2 + G_BANKS
 
+
+def square_form(unit):
+    return unit % GROUP_UNITS == 0
+
+
 FLOPS = 2 * 2 * SCENES * OBJECTS * OBJECTS * CHANNELS * OUT_CHANNELS
 BYTES = SCENES * OBJECTS * OBJECTS * (CHANNELS * (4 + 2) + OUT_CHANNELS * 4) + 2 * OUT_CHANNELS * CHANNELS * 2
 
@@ -183,6 +188,10 @@ def tile_differentiablelogicmachine_pa_v_kernel(tc, x1, x2, W2, b2, z, grad_out,
             nc.scalar.activation(
                 out=sigmoid_tiles[unit][:, cols, :], in_=zT[:].rearrange("p t c -> p c t"), func=ACT.Sigmoid
             )
+            if part == UNIT_BLOCKS - 1 and square_form(unit):
+                weighted = work.tile([P, UNIT_TOKENS, PACK], F32)
+                weighted_tiles[unit] = weighted
+                nc.scalar.activation(out=weighted[:], in_=sigmoid_tiles[unit][:], func=ACT.Square, bias=-0.5)
 
         def weigh(unit):
             weighted = work.tile([P, UNIT_TOKENS, PACK], F32)
@@ -190,7 +199,7 @@ def tile_differentiablelogicmachine_pa_v_kernel(tc, x1, x2, W2, b2, z, grad_out,
             nc.vector.scalar_tensor_tensor(
                 out=weighted[:],
                 in0=sigmoid_tiles[unit][:],
-                scalar=-1.0,
+                scalar=1.0,
                 in1=gT_tiles[unit][:].rearrange("p t c -> p c t"),
                 op0=ALU.mult,
                 op1=ALU.mult,
@@ -201,14 +210,25 @@ def tile_differentiablelogicmachine_pa_v_kernel(tc, x1, x2, W2, b2, z, grad_out,
             if unit_in_half == 0:
                 grouped = regroup.tile([P, HALF_TOKENS, PACK], BF16, align_bytes=64)
                 grouped_tiles[half] = grouped
-            nc.vector.scalar_tensor_tensor(
-                out=grouped_tiles[half][:, unit_in_half * UNIT_TOKENS : (unit_in_half + 1) * UNIT_TOKENS, :],
-                in0=sigmoid_tiles[unit][:],
-                scalar=1.0,
-                in1=weighted_tiles[unit][:],
-                op0=ALU.subtract,
-                op1=ALU.mult,
-            )
+            dst = grouped_tiles[half][:, unit_in_half * UNIT_TOKENS : (unit_in_half + 1) * UNIT_TOKENS, :]
+            if square_form(unit):
+                nc.vector.scalar_tensor_tensor(
+                    out=dst,
+                    in0=weighted_tiles[unit][:],
+                    scalar=0.25,
+                    in1=gT_tiles[unit][:].rearrange("p t c -> p c t"),
+                    op0=ALU.subtract,
+                    op1=ALU.mult,
+                )
+            else:
+                nc.vector.scalar_tensor_tensor(
+                    out=dst,
+                    in0=sigmoid_tiles[unit][:],
+                    scalar=1.0,
+                    in1=weighted_tiles[unit][:],
+                    op0=ALU.subtract,
+                    op1=ALU.mult,
+                )
 
         def quantise_half(half):
             group, side = divmod(half, GROUP_HALVES)
@@ -261,7 +281,7 @@ def tile_differentiablelogicmachine_pa_v_kernel(tc, x1, x2, W2, b2, z, grad_out,
                 start=False,
                 stop=True,
             )
-            nc.scalar.copy(out=result_tiles[store][:, slot, :], in_=acc[:])
+            nc.scalar.activation(out=result_tiles[store][:, slot, :], in_=acc[:], func=ACT.Copy, scale=-1.0)
             if slot == STORE_BLOCKS - 1:
                 nc.sync.dma_start(
                     out=out_stores[group, store % GROUP_STORES],
@@ -270,14 +290,16 @@ def tile_differentiablelogicmachine_pa_v_kernel(tc, x1, x2, W2, b2, z, grad_out,
 
         def vector_round(unit):
             finished = unit - 1
-            if unit < UNITS:
+            if unit < UNITS and not square_form(unit):
                 weigh(unit)
             if finished > 0 and finished % HALF_UNITS == 0:
                 quantise_half(finished // HALF_UNITS - 1)
-            if 0 <= finished < UNITS:
+            if 0 <= finished < UNITS and not square_form(finished):
                 gradient(finished)
             if finished > 0 and finished % GROUP_UNITS == 0:
                 swap_objects(finished // GROUP_UNITS - 1)
+            if unit < UNITS and square_form(unit):
+                gradient(unit)
 
         for unit in range(UNITS + LAG_UNITS):
             if unit < UNITS:

@@ -41,6 +41,7 @@ WEIGHT_CHUNKS = OUT_CHANNELS // P
 BANK_CHUNKS = 2
 WEIGHT_BANKS = WEIGHT_CHUNKS // BANK_CHUNKS
 
+WORDS = 2
 LOAD_BUFS = 12
 LEAD_UNITS = 4
 WORK_BUFS = 3
@@ -53,7 +54,7 @@ LAG_UNITS = GROUP_UNITS + 2 + G_BANKS
 
 
 def square_form(unit):
-    return unit % GROUP_UNITS == 0
+    return False
 
 
 FLOPS = 2 * 2 * SCENES * OBJECTS * OBJECTS * CHANNELS * OUT_CHANNELS
@@ -88,15 +89,11 @@ def tile_differentiablelogicmachine_pa_v_kernel(tc, x1, x2, W2, b2, z, grad_out,
 
         ident_f32 = consts.tile([P, P], F32)
         make_identity(nc, ident_f32[:])
-        ident_bf = consts.tile([P, P], BF16)
-        nc.vector.tensor_copy(out=ident_bf[:], in_=ident_f32[:])
         perm_f32 = consts.tile([P, P], F32)
-        perm_bf = consts.tile([P, P], BF16)
-        for perm in (perm_f32, perm_bf):
-            nc.vector.tensor_copy(
-                out=perm[:].rearrange("p (x s) -> p x s", s=GROUP_SCENES),
-                in_=ident_f32[:].rearrange("p (s x) -> p x s", s=GROUP_SCENES),
-            )
+        nc.vector.tensor_copy(
+            out=perm_f32[:].rearrange("p (x s) -> p x s", s=GROUP_SCENES),
+            in_=ident_f32[:].rearrange("p (s x) -> p x s", s=GROUP_SCENES),
+        )
 
         z_tiles = []
         g_tiles = []
@@ -146,17 +143,16 @@ def tile_differentiablelogicmachine_pa_v_kernel(tc, x1, x2, W2, b2, z, grad_out,
         def weight_bank(index):
             w_rows, w_grouped, codes, scales = weight_operands[index // WEIGHT_BANKS]
             bank = index % WEIGHT_BANKS
-            wT = psum_o.tile([P, PACK, UNIT_TOKENS], BF16, tag="acc")
+            wT = psum_o.tile([P, BANK_CHUNKS, WORDS, P], F32, tag="acc")
             for n in range(BANK_CHUNKS):
-                for t in range(PACK):
-                    nc.tensor.transpose(
-                        wT[:, t, n * P : (n + 1) * P],
-                        w_rows[:, BANK_CHUNKS * bank + n, t * P : (t + 1) * P],
-                        ident_bf[:],
-                    )
+                words = w_rows[:, BANK_CHUNKS * bank + n, :].bitcast(F32)
+                for u in range(WORDS):
+                    nc.tensor.transpose(wT[:, n, u, :], words[:, u * P : (u + 1) * P], ident_f32[:])
+            flat = w_grouped[:].rearrange("p c t -> p (c t)")
+            piece = flat[:, bank * UNIT_TOKENS * PACK : (bank + 1) * UNIT_TOKENS * PACK].bitcast(F32)
             nc.scalar.copy(
-                out=w_grouped[:, bank * UNIT_TOKENS : (bank + 1) * UNIT_TOKENS, :],
-                in_=wT[:].rearrange("p t c -> p c t"),
+                out=piece.rearrange("p (n c u) -> p n c u", c=P, u=WORDS),
+                in_=wT[:].rearrange("p n u c -> p n c u"),
             )
             if bank == WEIGHT_BANKS - 1:
                 nc.vector.quantize_mx(
@@ -174,17 +170,19 @@ def tile_differentiablelogicmachine_pa_v_kernel(tc, x1, x2, W2, b2, z, grad_out,
             unit, part = divmod(block, UNIT_BLOCKS)
             if part == 0:
                 sigmoid = work.tile([P, UNIT_TOKENS, PACK], F32)
-                gT = psum_g.tile([P, PACK, UNIT_TOKENS], BF16)
+                gT = psum_g.tile([P, WORDS, UNIT_TOKENS], F32)
                 sigmoid_tiles[unit] = sigmoid
                 gT_tiles[unit] = gT
             cols = slice(part * P, (part + 1) * P)
             zT = psum_z.tile([P, PACK, P], F32)
             for t in range(PACK):
-                nc.tensor.transpose(zT[:, t, :], z_tiles[unit][:, part, t * P : (t + 1) * P], perm_f32[:])
-            for t in range(PACK):
+                u, e = divmod(t, WORDS)
                 nc.tensor.transpose(
-                    gT_tiles[unit][:, t, cols], g_tiles[unit][:, part, t * P : (t + 1) * P], perm_bf[:]
+                    zT[:, t, :], z_tiles[unit][:, part, u * WORDS * P + e : (u + 1) * WORDS * P : WORDS], perm_f32[:]
                 )
+            g_words = g_tiles[unit][:, part, :].bitcast(F32)
+            for u in range(WORDS):
+                nc.tensor.transpose(gT_tiles[unit][:, u, cols], g_words[:, u * P : (u + 1) * P], perm_f32[:])
             nc.scalar.activation(
                 out=sigmoid_tiles[unit][:, cols, :], in_=zT[:].rearrange("p t c -> p c t"), func=ACT.Sigmoid
             )
@@ -196,13 +194,11 @@ def tile_differentiablelogicmachine_pa_v_kernel(tc, x1, x2, W2, b2, z, grad_out,
         def weigh(unit):
             weighted = work.tile([P, UNIT_TOKENS, PACK], F32)
             weighted_tiles[unit] = weighted
-            nc.vector.scalar_tensor_tensor(
-                out=weighted[:],
-                in0=sigmoid_tiles[unit][:],
-                scalar=1.0,
-                in1=gT_tiles[unit][:].rearrange("p t c -> p c t"),
-                op0=ALU.mult,
-                op1=ALU.mult,
+            nc.vector.tensor_tensor(
+                out=weighted[:].rearrange("p c (u e) -> p c u e", e=WORDS),
+                in0=sigmoid_tiles[unit][:].rearrange("p c (u e) -> p c u e", e=WORDS),
+                in1=gT_tiles[unit][:].rearrange("p u c -> p (u c)").bitcast(BF16).rearrange("p (u c e) -> p c u e", u=WORDS, e=WORDS),
+                op=ALU.mult,
             )
 
         def gradient(unit):
@@ -213,10 +209,10 @@ def tile_differentiablelogicmachine_pa_v_kernel(tc, x1, x2, W2, b2, z, grad_out,
             dst = grouped_tiles[half][:, unit_in_half * UNIT_TOKENS : (unit_in_half + 1) * UNIT_TOKENS, :]
             if square_form(unit):
                 nc.vector.scalar_tensor_tensor(
-                    out=dst,
-                    in0=weighted_tiles[unit][:],
+                    out=dst.rearrange("p c (u e) -> p c u e", e=WORDS),
+                    in0=weighted_tiles[unit][:].rearrange("p c (u e) -> p c u e", e=WORDS),
                     scalar=0.25,
-                    in1=gT_tiles[unit][:].rearrange("p t c -> p c t"),
+                    in1=gT_tiles[unit][:].rearrange("p u c -> p (u c)").bitcast(BF16).rearrange("p (u c e) -> p c u e", u=WORDS, e=WORDS),
                     op0=ALU.subtract,
                     op1=ALU.mult,
                 )

@@ -54,7 +54,7 @@ LAG_UNITS = GROUP_UNITS + 2 + G_BANKS
 
 
 def square_form(unit):
-    return False
+    return unit % GROUP_UNITS == 0
 
 
 FLOPS = 2 * 2 * SCENES * OBJECTS * OBJECTS * CHANNELS * OUT_CHANNELS
@@ -170,7 +170,7 @@ def tile_differentiablelogicmachine_pa_v_kernel(tc, x1, x2, W2, b2, z, grad_out,
             unit, part = divmod(block, UNIT_BLOCKS)
             if part == 0:
                 sigmoid = work.tile([P, UNIT_TOKENS, PACK], F32)
-                gT = psum_g.tile([P, WORDS, UNIT_TOKENS], F32)
+                gT = psum_g.tile([P, UNIT_TOKENS, WORDS], F32)
                 sigmoid_tiles[unit] = sigmoid
                 gT_tiles[unit] = gT
             cols = slice(part * P, (part + 1) * P)
@@ -182,7 +182,7 @@ def tile_differentiablelogicmachine_pa_v_kernel(tc, x1, x2, W2, b2, z, grad_out,
                 )
             g_words = g_tiles[unit][:, part, :].bitcast(F32)
             for u in range(WORDS):
-                nc.tensor.transpose(gT_tiles[unit][:, u, cols], g_words[:, u * P : (u + 1) * P], perm_f32[:])
+                nc.tensor.transpose(gT_tiles[unit][:, cols, u], g_words[:, u * P : (u + 1) * P], perm_f32[:])
             nc.scalar.activation(
                 out=sigmoid_tiles[unit][:, cols, :], in_=zT[:].rearrange("p t c -> p c t"), func=ACT.Sigmoid
             )
@@ -195,9 +195,9 @@ def tile_differentiablelogicmachine_pa_v_kernel(tc, x1, x2, W2, b2, z, grad_out,
             weighted = work.tile([P, UNIT_TOKENS, PACK], F32)
             weighted_tiles[unit] = weighted
             nc.vector.tensor_tensor(
-                out=weighted[:].rearrange("p c (u e) -> p c u e", e=WORDS),
-                in0=sigmoid_tiles[unit][:].rearrange("p c (u e) -> p c u e", e=WORDS),
-                in1=gT_tiles[unit][:].rearrange("p u c -> p (u c)").bitcast(BF16).rearrange("p (u c e) -> p c u e", u=WORDS, e=WORDS),
+                out=weighted[:].rearrange("p c t -> p (c t)"),
+                in0=sigmoid_tiles[unit][:].rearrange("p c t -> p (c t)"),
+                in1=gT_tiles[unit][:].rearrange("p c u -> p (c u)").bitcast(BF16),
                 op=ALU.mult,
             )
 
@@ -209,10 +209,10 @@ def tile_differentiablelogicmachine_pa_v_kernel(tc, x1, x2, W2, b2, z, grad_out,
             dst = grouped_tiles[half][:, unit_in_half * UNIT_TOKENS : (unit_in_half + 1) * UNIT_TOKENS, :]
             if square_form(unit):
                 nc.vector.scalar_tensor_tensor(
-                    out=dst.rearrange("p c (u e) -> p c u e", e=WORDS),
-                    in0=weighted_tiles[unit][:].rearrange("p c (u e) -> p c u e", e=WORDS),
+                    out=dst.rearrange("p c t -> p (c t)"),
+                    in0=weighted_tiles[unit][:].rearrange("p c t -> p (c t)"),
                     scalar=0.25,
-                    in1=gT_tiles[unit][:].rearrange("p u c -> p (u c)").bitcast(BF16).rearrange("p (u c e) -> p c u e", u=WORDS, e=WORDS),
+                    in1=gT_tiles[unit][:].rearrange("p c u -> p (c u)").bitcast(BF16),
                     op0=ALU.subtract,
                     op1=ALU.mult,
                 )

@@ -53,8 +53,15 @@ OUT_BANKS = 3
 LAG_UNITS = GROUP_UNITS + 2 + G_BANKS
 
 
+SQUARE_UNITS = (0, 2, 4, 6, 8, 12)
+SPLIT_UNITS = 1
+VECTOR_FROM = 24
+LAST_SINGLE = 8
+RUN_UNITS = 1
+
+
 def square_form(unit):
-    return unit % GROUP_UNITS == 0
+    return unit in SQUARE_UNITS
 
 
 FLOPS = 2 * 2 * SCENES * OBJECTS * OBJECTS * CHANNELS * OUT_CHANNELS
@@ -72,6 +79,10 @@ def tile_differentiablelogicmachine_pa_v_kernel(tc, x1, x2, W2, b2, z, grad_out,
     )
     out_stores = out.rearrange("b i j c -> (b i j) c").rearrange(
         "(q s x n r) c -> q n x s (r c)", q=GROUPS, s=GROUP_SCENES, x=PAIRS, n=GROUP_STORES, r=STORE_BLOCKS
+    )
+
+    out_single = out.rearrange("b i j c -> (b i j) c").rearrange(
+        "(q s x n) c -> q n x s c", q=GROUPS, s=GROUP_SCENES, x=PAIRS, n=GROUP_BLOCKS
     )
 
     with ExitStack() as ctx:
@@ -101,9 +112,14 @@ def tile_differentiablelogicmachine_pa_v_kernel(tc, x1, x2, W2, b2, z, grad_out,
         def load_unit(unit):
             group, unit_in_group = divmod(unit, GROUP_UNITS)
             z_tile = loads.tile([P, UNIT_BLOCKS, CHANNELS], F32)
-            nc.sync.dma_start(out=z_tile[:], in_=z_units[group, unit_in_group])
             g_tile = loads.tile([P, UNIT_BLOCKS, CHANNELS], BF16)
-            nc.sync.dma_start(out=g_tile[:], in_=g_units[group, unit_in_group])
+            if unit < SPLIT_UNITS:
+                for part in range(UNIT_BLOCKS):
+                    nc.sync.dma_start(out=z_tile[:, part, :], in_=z_units[group, unit_in_group][:, part, :])
+                    nc.sync.dma_start(out=g_tile[:, part, :], in_=g_units[group, unit_in_group][:, part, :])
+            else:
+                nc.sync.dma_start(out=z_tile[:], in_=z_units[group, unit_in_group])
+                nc.sync.dma_start(out=g_tile[:], in_=g_units[group, unit_in_group])
             z_tiles.append(z_tile)
             g_tiles.append(g_tile)
 
@@ -254,6 +270,7 @@ def tile_differentiablelogicmachine_pa_v_kernel(tc, x1, x2, W2, b2, z, grad_out,
         def product_block(block):
             group, block_in_group = divmod(block, GROUP_BLOCKS)
             store, slot = divmod(block, STORE_BLOCKS)
+            single = block >= BLOCKS - LAST_SINGLE
             if slot == 0:
                 result = results.tile([P, STORE_BLOCKS, OUT_CHANNELS], F32)
                 result_tiles[store] = result
@@ -277,8 +294,13 @@ def tile_differentiablelogicmachine_pa_v_kernel(tc, x1, x2, W2, b2, z, grad_out,
                 start=False,
                 stop=True,
             )
-            nc.scalar.activation(out=result_tiles[store][:, slot, :], in_=acc[:], func=ACT.Copy, scale=-1.0)
-            if slot == STORE_BLOCKS - 1:
+            if block >= VECTOR_FROM and block % 2 == 1:
+                nc.vector.tensor_scalar_mul(out=result_tiles[store][:, slot, :], in0=acc[:], scalar1=-1.0)
+            else:
+                nc.scalar.activation(out=result_tiles[store][:, slot, :], in_=acc[:], func=ACT.Copy, scale=-1.0)
+            if single:
+                nc.sync.dma_start(out=out_single[group, block_in_group], in_=result_tiles[store][:, slot, :])
+            elif slot == STORE_BLOCKS - 1:
                 nc.sync.dma_start(
                     out=out_stores[group, store % GROUP_STORES],
                     in_=result_tiles[store][:].rearrange("p r c -> p (r c)"),
@@ -305,6 +327,8 @@ def tile_differentiablelogicmachine_pa_v_kernel(tc, x1, x2, W2, b2, z, grad_out,
                 vector_round(unit)
             if 0 <= unit + 1 - LEAD_UNITS < 2 * WEIGHT_BANKS:
                 weight_bank(unit + 1 - LEAD_UNITS)
-            if unit >= LAG_UNITS:
-                for part in range(UNIT_BLOCKS):
-                    product_block((unit - LAG_UNITS) * UNIT_BLOCKS + part)
+            if unit >= LAG_UNITS and (unit >= UNITS or (unit - LAG_UNITS) % RUN_UNITS == RUN_UNITS - 1):
+                span = 1 if unit >= UNITS else RUN_UNITS
+                for n in range(span):
+                    for part in range(UNIT_BLOCKS):
+                        product_block((unit - LAG_UNITS - span + 1 + n) * UNIT_BLOCKS + part)

@@ -44,11 +44,11 @@ WEIGHT_BANKS = WEIGHT_CHUNKS // BANK_CHUNKS
 WORDS = 2
 LOAD_BUFS = 12
 LEAD_UNITS = 4
-WORK_BUFS = 3
+WORK_BUFS = 4
 REGROUP_BUFS = 3
 RESULT_BUFS = 6
-Z_BANKS = 3
-G_BANKS = 2
+Z_BANKS = 2
+G_BANKS = 3
 OUT_BANKS = 3
 LAG_UNITS = GROUP_UNITS + 2 + G_BANKS
 
@@ -251,19 +251,33 @@ def tile_differentiablelogicmachine_pa_v_kernel(tc, x1, x2, W2, b2, z, grad_out,
                 in_=grouped_tiles[half][:].rearrange("p c t -> p (c t)"),
             )
 
-        def swap_objects(group):
+        def quantise_unit(unit):
+            group, unit_in_group = divmod(unit, GROUP_UNITS)
+            half, unit_in_half = divmod(unit, HALF_UNITS)
+            cols = slice(unit_in_group * UNIT_TOKENS, (unit_in_group + 1) * UNIT_TOKENS)
+            nc.vector.quantize_mx(
+                out=dz_codes[:, group, cols].bitcast(E5M2X4),
+                scales=dz_scales[:, group, cols],
+                in_=grouped_tiles[half][:, unit_in_half * UNIT_TOKENS : (unit_in_half + 1) * UNIT_TOKENS, :].rearrange(
+                    "p c t -> p (c t)"
+                ),
+            )
+
+        def swap_objects(group, first=0, last=GROUP_BLOCKS):
             split = "p (jl ih il jh s) -> p jl ih il jh s"
             sizes = dict(jl=8, ih=2, il=8, jh=2)
             src = dz_codes[:, group, :].bitcast(I32).rearrange(split, s=GROUP_SCENES, **sizes)
             dst = swap_codes[:, group, :].bitcast(I32).rearrange(split, s=GROUP_SCENES, **sizes)
             for ih in range(2):
                 nc.vector.tensor_copy(
-                    out=dst[:, :, ih, :, :, :],
-                    in_=src[:, :, :, :, ih, :].rearrange("p il jh jl s -> p jl il jh s"),
+                    out=dst[:, :, ih, first:last, :, :],
+                    in_=src[:, first:last, :, :, ih, :].rearrange("p il jh jl s -> p jl il jh s"),
                 )
             src = dz_scales[:, group, :].bitcast(I32).rearrange("p (jl ih il jh) -> p jl ih il jh", **sizes)
             dst = swap_scales[:, group, :].bitcast(I32).rearrange("p (jl ih il jh) -> p jl ih il jh", **sizes)
-            nc.vector.tensor_copy(out=dst, in_=src.rearrange("p il jh jl ih -> p jl ih il jh"))
+            nc.vector.tensor_copy(
+                out=dst[:, :, :, first:last, :], in_=src[:, first:last, :, :, :].rearrange("p il jh jl ih -> p jl ih il jh")
+            )
 
         result_tiles = {}
 
@@ -310,11 +324,18 @@ def tile_differentiablelogicmachine_pa_v_kernel(tc, x1, x2, W2, b2, z, grad_out,
             finished = unit - 1
             if unit < UNITS and not square_form(unit):
                 weigh(unit)
-            if finished > 0 and finished % HALF_UNITS == 0:
+            if unit == UNITS:
+                swap_objects(GROUPS - 1, 0, GROUP_BLOCKS // 2)
+                quantise_unit(UNITS - 2)
+            elif unit == UNITS + 1:
+                swap_objects(GROUPS - 1, GROUP_BLOCKS // 2, GROUP_BLOCKS - UNIT_BLOCKS)
+                quantise_unit(UNITS - 1)
+                swap_objects(GROUPS - 1, GROUP_BLOCKS - UNIT_BLOCKS, GROUP_BLOCKS)
+            elif finished > 0 and finished % HALF_UNITS == 0:
                 quantise_half(finished // HALF_UNITS - 1)
             if 0 <= finished < UNITS and not square_form(finished):
                 gradient(finished)
-            if finished > 0 and finished % GROUP_UNITS == 0:
+            if 0 < finished < UNITS and finished % GROUP_UNITS == 0:
                 swap_objects(finished // GROUP_UNITS - 1)
             if unit < UNITS and square_form(unit):
                 gradient(unit)

from contextlib import ExitStack

import concourse.mybir as mybir
from concourse.masks import make_identity

F32 = mybir.dt.float32
BF16 = mybir.dt.bfloat16
I32 = mybir.dt.int32
U32 = mybir.dt.uint32
U8 = mybir.dt.uint8
E5M2X4 = mybir.dt.float8_e5m2_x4
E4M3X4 = mybir.dt.float8_e4m3fn_x4
ACT = mybir.ActivationFunctionType
ALU = mybir.AluOpType

P = 128
PACK = 4
SCENES = 16
OBJECTS = 16
CHANNELS = 512
OUT_CHANNELS = 512
WB_FIRST_ROW = 512
WD_FIRST_ROW = 1536

GROUP_SCENES = 4
GROUPS = SCENES // GROUP_SCENES
GROUP_TOKENS = GROUP_SCENES * OBJECTS * OBJECTS
GROUP_BLOCKS = GROUP_TOKENS // P
BLOCKS = GROUPS * GROUP_BLOCKS
UNIT_BLOCKS = 2
UNIT_TOKENS = UNIT_BLOCKS * P
UNITS = BLOCKS // UNIT_BLOCKS
GROUP_UNITS = GROUP_BLOCKS // UNIT_BLOCKS
GROUP_HALVES = 2
HALF_UNITS = GROUP_UNITS // GROUP_HALVES
HALF_TOKENS = GROUP_TOKENS // GROUP_HALVES
STORE_BLOCKS = 2
GROUP_STORES = GROUP_BLOCKS // STORE_BLOCKS
PAIRS = P // GROUP_SCENES
WEIGHT_CHUNKS = OUT_CHANNELS // P
BANK_CHUNKS = 2
WEIGHT_BANKS = WEIGHT_CHUNKS // BANK_CHUNKS

WORDS = 2
LOAD_BUFS = 12
LEAD_UNITS = 4
WORK_BUFS = 4
REGROUP_BUFS = 3
RESULT_BUFS = 6
Z_BANKS = 2
G_BANKS = 3
OUT_BANKS = 3
LAG_UNITS = GROUP_UNITS + 2 + G_BANKS


SQUARE_UNITS = (0, 2, 4, 6, 8, 12)
SPLIT_UNITS = 1
VECTOR_FROM = 24
LAST_SINGLE = 8
RUN_UNITS = 1


def square_form(unit):
    return unit in SQUARE_UNITS


FLOPS = 2 * 2 * SCENES * OBJECTS * OBJECTS * CHANNELS * OUT_CHANNELS
BYTES = SCENES * OBJECTS * OBJECTS * (CHANNELS * (4 + 2) + OUT_CHANNELS * 4) + 2 * OUT_CHANNELS * CHANNELS * 2


def tile_differentiablelogicmachine_pa_v_kernel(tc, x1, x2, W2, b2, z, grad_out, out):
    nc = tc.nc

    z_units = z.rearrange("b i j o -> (b i j) o").rearrange(
        "(q p u r) o -> q u p r o", q=GROUPS, p=P, u=GROUP_UNITS, r=UNIT_BLOCKS
    )
    g_units = grad_out.rearrange("b i j o -> (b i j) o").rearrange(
        "(q p u r) o -> q u p r o", q=GROUPS, p=P, u=GROUP_UNITS, r=UNIT_BLOCKS
    )
    out_stores = out.rearrange("b i j c -> (b i j) c").rearrange(
        "(q s x n r) c -> q n x s (r c)", q=GROUPS, s=GROUP_SCENES, x=PAIRS, n=GROUP_STORES, r=STORE_BLOCKS
    )

    out_single = out.rearrange("b i j c -> (b i j) c").rearrange(
        "(q s x n) c -> q n x s c", q=GROUPS, s=GROUP_SCENES, x=PAIRS, n=GROUP_BLOCKS
    )

    with ExitStack() as ctx:
        ctx.enter_context(tc.manual_schedule())
        consts = ctx.enter_context(tc.tile_pool(name="consts", bufs=1))
        weights = ctx.enter_context(tc.tile_pool(name="weights", bufs=1))
        loads = ctx.enter_context(tc.tile_pool(name="loads", bufs=LOAD_BUFS))
        work = ctx.enter_context(tc.tile_pool(name="work", bufs=WORK_BUFS))
        regroup = ctx.enter_context(tc.tile_pool(name="regroup", bufs=REGROUP_BUFS))
        keep = ctx.enter_context(tc.tile_pool(name="keep", bufs=1))
        results = ctx.enter_context(tc.tile_pool(name="results", bufs=RESULT_BUFS))
        psum_z = ctx.enter_context(tc.psum_pool(name="psum_z", bufs=Z_BANKS))
        psum_g = ctx.enter_context(tc.psum_pool(name="psum_g", bufs=G_BANKS))
        psum_o = ctx.enter_context(tc.psum_pool(name="psum_o", bufs=OUT_BANKS))

        ident_f32 = consts.tile([P, P], F32)
        make_identity(nc, ident_f32[:])
        perm_f32 = consts.tile([P, P], F32)
        nc.vector.tensor_copy(
            out=perm_f32[:].rearrange("p (x s) -> p x s", s=GROUP_SCENES),
            in_=ident_f32[:].rearrange("p (s x) -> p x s", s=GROUP_SCENES),
        )

        z_tiles = []
        g_tiles = []

        def load_unit(unit):
            group, unit_in_group = divmod(unit, GROUP_UNITS)
            z_tile = loads.tile([P, UNIT_BLOCKS, CHANNELS], F32)
            g_tile = loads.tile([P, UNIT_BLOCKS, CHANNELS], BF16)
            if unit < SPLIT_UNITS:
                for part in range(UNIT_BLOCKS):
                    nc.sync.dma_start(out=z_tile[:, part, :], in_=z_units[group, unit_in_group][:, part, :])
                    nc.sync.dma_start(out=g_tile[:, part, :], in_=g_units[group, unit_in_group][:, part, :])
            else:
                nc.sync.dma_start(out=z_tile[:], in_=z_units[group, unit_in_group])
                nc.sync.dma_start(out=g_tile[:], in_=g_units[group, unit_in_group])
            z_tiles.append(z_tile)
            g_tiles.append(g_tile)

        def load_weight(first_row, name):
            w_rows = weights.tile([P, WEIGHT_CHUNKS, CHANNELS], BF16, name=name)
            nc.sync.dma_start(
                out=w_rows[:],
                in_=W2[first_row : first_row + OUT_CHANNELS, :].rearrange("(n p) o -> p n o", p=P),
            )
            return w_rows

        for unit in range(LEAD_UNITS):
            load_unit(unit)
        wb_rows = load_weight(WB_FIRST_ROW, "wb_rows")
        wd_rows = load_weight(WD_FIRST_ROW, "wd_rows")
        for unit in range(LEAD_UNITS, UNITS):
            load_unit(unit)

        dz_codes = keep.tile([P, GROUPS, GROUP_TOKENS], U32, align_bytes=64)
        dz_scales = keep.tile([P, GROUPS, GROUP_TOKENS], U8, align_bytes=64)
        swap_codes = keep.tile([P, GROUPS, GROUP_TOKENS], U32, align_bytes=64)
        swap_scales = keep.tile([P, GROUPS, GROUP_TOKENS], U8, align_bytes=64)
        nc.vector.memset(dz_scales[:].rearrange("p q n -> p (q n)").bitcast(I32), 0)

        wb_codes = keep.tile([P, OUT_CHANNELS], U32, align_bytes=64)
        wb_scales = keep.tile([P, OUT_CHANNELS], U8, align_bytes=64)
        wd_codes = keep.tile([P, OUT_CHANNELS], U32, align_bytes=64)
        wd_scales = keep.tile([P, OUT_CHANNELS], U8, align_bytes=64)

        wb_grouped = weights.tile([P, OUT_CHANNELS, PACK], BF16, align_bytes=64)
        wd_grouped = weights.tile([P, OUT_CHANNELS, PACK], BF16, align_bytes=64)
        weight_operands = (
            (wb_rows, wb_grouped, wb_codes, wb_scales),
            (wd_rows, wd_grouped, wd_codes, wd_scales),
        )

        def weight_bank(index):
            w_rows, w_grouped, codes, scales = weight_operands[index // WEIGHT_BANKS]
            bank = index % WEIGHT_BANKS
            wT = psum_o.tile([P, BANK_CHUNKS, WORDS, P], F32, tag="acc")
            for n in range(BANK_CHUNKS):
                words = w_rows[:, BANK_CHUNKS * bank + n, :].bitcast(F32)
                for u in range(WORDS):
                    nc.tensor.transpose(wT[:, n, u, :], words[:, u * P : (u + 1) * P], ident_f32[:])
            flat = w_grouped[:].rearrange("p c t -> p (c t)")
            piece = flat[:, bank * UNIT_TOKENS * PACK : (bank + 1) * UNIT_TOKENS * PACK].bitcast(F32)
            nc.scalar.copy(
                out=piece.rearrange("p (n c u) -> p n c u", c=P, u=WORDS),
                in_=wT[:].rearrange("p n u c -> p n c u"),
            )
            if bank == WEIGHT_BANKS - 1:
                nc.vector.quantize_mx(
                    out=codes[:].bitcast(E4M3X4),
                    scales=scales[:],
                    in_=w_grouped[:].rearrange("p c t -> p (c t)"),
                )

        sigmoid_tiles = {}
        gT_tiles = {}
        weighted_tiles = {}
        grouped_tiles = {}

        def transpose_block(block):
            unit, part = divmod(block, UNIT_BLOCKS)
            if part == 0:
                sigmoid = work.tile([P, UNIT_TOKENS, PACK], F32)
                gT = psum_g.tile([P, UNIT_TOKENS, WORDS], F32)
                sigmoid_tiles[unit] = sigmoid
                gT_tiles[unit] = gT
            cols = slice(part * P, (part + 1) * P)
            zT = psum_z.tile([P, PACK, P], F32)
            for t in range(PACK):
                u, e = divmod(t, WORDS)
                nc.tensor.transpose(
                    zT[:, t, :], z_tiles[unit][:, part, u * WORDS * P + e : (u + 1) * WORDS * P : WORDS], perm_f32[:]
                )
            g_words = g_tiles[unit][:, part, :].bitcast(F32)
            for u in range(WORDS):
                nc.tensor.transpose(gT_tiles[unit][:, cols, u], g_words[:, u * P : (u + 1) * P], perm_f32[:])
            nc.scalar.activation(
                out=sigmoid_tiles[unit][:, cols, :], in_=zT[:].rearrange("p t c -> p c t"), func=ACT.Sigmoid
            )
            if part == UNIT_BLOCKS - 1 and square_form(unit):
                weighted = work.tile([P, UNIT_TOKENS, PACK], F32)
                weighted_tiles[unit] = weighted
                nc.scalar.activation(out=weighted[:], in_=sigmoid_tiles[unit][:], func=ACT.Square, bias=-0.5)

        def weigh(unit):
            weighted = work.tile([P, UNIT_TOKENS, PACK], F32)
            weighted_tiles[unit] = weighted
            nc.vector.tensor_tensor(
                out=weighted[:].rearrange("p c t -> p (c t)"),
                in0=sigmoid_tiles[unit][:].rearrange("p c t -> p (c t)"),
                in1=gT_tiles[unit][:].rearrange("p c u -> p (c u)").bitcast(BF16),
                op=ALU.mult,
            )

        def gradient(unit):
            half, unit_in_half = divmod(unit, HALF_UNITS)
            if unit_in_half == 0:
                grouped = regroup.tile([P, HALF_TOKENS, PACK], BF16, align_bytes=64)
                grouped_tiles[half] = grouped
            dst = grouped_tiles[half][:, unit_in_half * UNIT_TOKENS : (unit_in_half + 1) * UNIT_TOKENS, :]
            if square_form(unit):
                nc.vector.scalar_tensor_tensor(
                    out=dst.rearrange("p c t -> p (c t)"),
                    in0=weighted_tiles[unit][:].rearrange("p c t -> p (c t)"),
                    scalar=0.25,
                    in1=gT_tiles[unit][:].rearrange("p c u -> p (c u)").bitcast(BF16),
                    op0=ALU.subtract,
                    op1=ALU.mult,
                )
            else:
                nc.vector.scalar_tensor_tensor(
                    out=dst,
                    in0=sigmoid_tiles[unit][:],
                    scalar=1.0,
                    in1=weighted_tiles[unit][:],
                    op0=ALU.subtract,
                    op1=ALU.mult,
                )

        def quantise_half(half):
            group, side = divmod(half, GROUP_HALVES)
            cols = slice(side * HALF_TOKENS, (side + 1) * HALF_TOKENS)
            nc.vector.quantize_mx(
                out=dz_codes[:, group, cols].bitcast(E5M2X4),
                scales=dz_scales[:, group, cols],
                in_=grouped_tiles[half][:].rearrange("p c t -> p (c t)"),
            )

        def quantise_unit(unit):
            group, unit_in_group = divmod(unit, GROUP_UNITS)
            half, unit_in_half = divmod(unit, HALF_UNITS)
            cols = slice(unit_in_group * UNIT_TOKENS, (unit_in_group + 1) * UNIT_TOKENS)
            nc.vector.quantize_mx(
                out=dz_codes[:, group, cols].bitcast(E5M2X4),
                scales=dz_scales[:, group, cols],
                in_=grouped_tiles[half][:, unit_in_half * UNIT_TOKENS : (unit_in_half + 1) * UNIT_TOKENS, :].rearrange(
                    "p c t -> p (c t)"
                ),
            )

        def swap_objects(group, first=0, last=GROUP_BLOCKS):
            split = "p (jl ih il jh s) -> p jl ih il jh s"
            sizes = dict(jl=8, ih=2, il=8, jh=2)
            src = dz_codes[:, group, :].bitcast(I32).rearrange(split, s=GROUP_SCENES, **sizes)
            dst = swap_codes[:, group, :].bitcast(I32).rearrange(split, s=GROUP_SCENES, **sizes)
            for ih in range(2):
                nc.vector.tensor_copy(
                    out=dst[:, :, ih, first:last, :, :],
                    in_=src[:, first:last, :, :, ih, :].rearrange("p il jh jl s -> p jl il jh s"),
                )
            src = dz_scales[:, group, :].bitcast(I32).rearrange("p (jl ih il jh) -> p jl ih il jh", **sizes)
            dst = swap_scales[:, group, :].bitcast(I32).rearrange("p (jl ih il jh) -> p jl ih il jh", **sizes)
            nc.vector.tensor_copy(
                out=dst[:, :, :, first:last, :], in_=src[:, first:last, :, :, :].rearrange("p il jh jl ih -> p jl ih il jh")
            )

        result_tiles = {}

        def product_block(block):
            group, block_in_group = divmod(block, GROUP_BLOCKS)
            store, slot = divmod(block, STORE_BLOCKS)
            single = block >= BLOCKS - LAST_SINGLE
            if slot == 0:
                result = results.tile([P, STORE_BLOCKS, OUT_CHANNELS], F32)
                result_tiles[store] = result
            cols = slice(block_in_group * P, (block_in_group + 1) * P)
            acc = psum_o.tile([P, OUT_CHANNELS], F32, tag="acc")
            nc.tensor.matmul_mx(
                out=acc[:],
                lhsT=dz_codes[:, group, cols].bitcast(E5M2X4),
                lhsT_scale=dz_scales[:, group, cols],
                rhs=wb_codes[:].bitcast(E4M3X4),
                rhs_scale=wb_scales[:],
                start=True,
                stop=False,
            )
            nc.tensor.matmul_mx(
                out=acc[:],
                lhsT=swap_codes[:, group, cols].bitcast(E5M2X4),
                lhsT_scale=swap_scales[:, group, cols],
                rhs=wd_codes[:].bitcast(E4M3X4),
                rhs_scale=wd_scales[:],
                start=False,
                stop=True,
            )
            if block >= VECTOR_FROM and block % 2 == 1:
                nc.vector.tensor_scalar_mul(out=result_tiles[store][:, slot, :], in0=acc[:], scalar1=-1.0)
            else:
                nc.scalar.activation(out=result_tiles[store][:, slot, :], in_=acc[:], func=ACT.Copy, scale=-1.0)
            if single:
                nc.sync.dma_start(out=out_single[group, block_in_group], in_=result_tiles[store][:, slot, :])
            elif slot == STORE_BLOCKS - 1:
                nc.sync.dma_start(
                    out=out_stores[group, store % GROUP_STORES],
                    in_=result_tiles[store][:].rearrange("p r c -> p (r c)"),
                )

        def vector_round(unit):
            finished = unit - 1
            if unit < UNITS and not square_form(unit):
                weigh(unit)
            if unit == UNITS:
                swap_objects(GROUPS - 1, 0, GROUP_BLOCKS // 2)
                quantise_unit(UNITS - 2)
            elif unit == UNITS + 1:
                swap_objects(GROUPS - 1, GROUP_BLOCKS // 2, GROUP_BLOCKS - UNIT_BLOCKS)
                quantise_unit(UNITS - 1)
                swap_objects(GROUPS - 1, GROUP_BLOCKS - UNIT_BLOCKS, GROUP_BLOCKS)
            elif finished > 0 and finished % HALF_UNITS == 0:
                quantise_half(finished // HALF_UNITS - 1)
            if 0 <= finished < UNITS and not square_form(finished):
                gradient(finished)
            if 0 < finished < UNITS and finished % GROUP_UNITS == 0:
                swap_objects(finished // GROUP_UNITS - 1)
            if unit < UNITS and square_form(unit):
                gradient(unit)

        for unit in range(UNITS + LAG_UNITS):
            if unit < UNITS:
                for part in range(UNIT_BLOCKS):
                    transpose_block(unit * UNIT_BLOCKS + part)
            if unit <= UNITS + 1:
                vector_round(unit)
            if 0 <= unit + 1 - LEAD_UNITS < 2 * WEIGHT_BANKS:
                weight_bank(unit + 1 - LEAD_UNITS)
            if unit >= LAG_UNITS and (unit >= UNITS or (unit - LAG_UNITS) % RUN_UNITS == RUN_UNITS - 1):
                span = 1 if unit >= UNITS else RUN_UNITS
                for n in range(span):
                    for part in range(UNIT_BLOCKS):
                        product_block((unit - LAG_UNITS - span + 1 + n) * UNIT_BLOCKS + part)
